import numpy as np
import ml_dtypes


def mxq(x, axis, fmt="e4m3"):
    dtype, down = {"e4m3": (ml_dtypes.float8_e4m3fn, 7), "e5m2": (ml_dtypes.float8_e5m2, 14)}[fmt]
    v = np.moveaxis(np.asarray(x, np.float32).astype(ml_dtypes.bfloat16).astype(np.float64), axis, -1)
    blocks = v.reshape(v.shape[:-1] + (-1, 32))
    amax = np.abs(blocks).max(-1, keepdims=True)
    byte = np.maximum(np.where(amax > 0, np.frexp(amax)[1] - 1 + 127, 0) - down, 1)
    scale = np.exp2(byte - 127.0)
    codes = (blocks / scale).astype(np.float32).astype(dtype).astype(np.float64)
    return np.moveaxis((codes * scale).reshape(v.shape), -1, axis)


WIDE = False


def mx_kscale(k):
    if not WIDE:
        return np.ones(k)
    levels = np.array([10, -10, 5, -5, 0])
    a = np.random.permutation(np.resize(levels, k // 512 * 4)).reshape(k // 512, 4)
    idx = np.arange(k)
    return np.exp2(a[idx // 512, idx % 128 // 32])


BF16 = ml_dtypes.bfloat16


def bf(x):
    return np.asarray(x, np.float32).astype(BF16)


def f64(x):
    return np.asarray(x).astype(np.float64)


E2M1 = np.array([0.0, 0.5, 1.0, 1.5, 2.0, 3.0, 4.0, 6.0, -0.0, -0.5, -1.0, -1.5, -2.0, -3.0, -4.0, -6.0])


def pack_weight(w, fmt):
    k, n = w.shape
    w = f64(bf(w)).reshape(k // 32, 32, n)
    amax = np.abs(w).max(1)
    if fmt == "e4m3":
        byte = np.frexp(amax)[1] - 1 + 127 - 7
    else:
        mant, ex = np.frexp(amax / 6.0)
        byte = np.where(mant > 0.5, ex, ex - 1) + 127
    byte = np.clip(np.where(amax > 0, byte, 1), 1, 254)
    scaled = (w * np.exp2(127.0 - byte)[:, None, :]).reshape(k, n).astype(np.float32)
    by_word = np.ascontiguousarray(scaled.reshape(k // 512, 128, 4, n).transpose(0, 1, 3, 2))
    if fmt == "e4m3":
        words = by_word.astype(ml_dtypes.float8_e4m3fn).view(np.uint8)
    else:
        c = by_word.astype(ml_dtypes.float4_e2m1fn).view(np.uint8) & 0xF
        words = c[..., 0::2] | (c[..., 1::2] << 4)
    return np.ascontiguousarray(words), np.ascontiguousarray(byte.astype(np.uint8).reshape(k // 512, 16, n))


def unpack_weight(words, scales, fmt):
    g, p, n, _ = words.shape
    if fmt == "e4m3":
        vals = np.ascontiguousarray(words).view(ml_dtypes.float8_e4m3fn).astype(np.float64)
    else:
        nib = np.empty((g, p, n, 4), np.uint8)
        nib[..., 0::2] = words & 0xF
        nib[..., 1::2] = words >> 4
        vals = E2M1[nib]
    vals = vals * np.repeat(np.exp2(scales.astype(np.float64) - 127.0), 8, axis=1)[..., None]
    return vals.transpose(0, 1, 3, 2).reshape(g * 512, n)

def pack4(w):
    words, scales = pack_weight(w, "e2m1")
    return words.reshape(words.shape[0], 128, -1), scales


def unpack4(words, scales):
    return unpack_weight(words.reshape(words.shape[0], 128, -1, 2), scales, "e2m1")


B, DS, HH, WW, HID, HL, REP, GRP = 4, 64, 64, 64, 128, 1024, 8, 4
C = 2 * DS
CN = REP * C


def elu(v):
    return np.where(v > 0.0, v, np.exp(np.minimum(v, 0.0)) - 1.0)


def neighbor_sum(x):
    xp = np.pad(x, ((0, 0), (0, 0), (1, 1), (1, 1)))
    full = sum(xp[:, :, di:di + HH, dj:dj + WW] for di in range(3) for dj in range(3))
    return full - x


def to_rows(t):
    return t.transpose(0, 2, 3, 1).reshape(B * HH * WW, t.shape[1])


def to_maps(r):
    return r.reshape(B, HH, WW, r.shape[1]).transpose(0, 3, 1, 2)


def setup_inputs():
    sc = mx_kscale(CN)[::REP]
    x_cat = bf(np.random.standard_normal((B, C, HH, WW)) * 0.4 * sc[None, :, None, None])
    w1 = np.random.standard_normal((HID, CN)) / np.sqrt(CN) / np.repeat(sc, REP)[None, :]
    words, scales = pack4(np.ascontiguousarray(w1.T))
    return {"x_cat": x_cat, "w1_words": words, "w1_scales": scales}


def reference(x_cat, w1_words, w1_scales):
    nbr = neighbor_sum(f64(x_cat))
    xn = np.repeat(nbr, REP, axis=1)
    z = mxq(to_rows(xn), 1, "e4m3") @ unpack4(w1_words, w1_scales)
    return to_maps(elu(z))

@@ -1,0 +1,365 @@
+from contextlib import ExitStack
+
+import concourse.mybir as mybir
+from concourse.masks import make_identity
+
+FLOPS = 2 * 4 * 64 * 64 * 1024 * 128
+
+BF16 = mybir.dt.bfloat16
+F32 = mybir.dt.float32
+I32 = mybir.dt.int32
+U32 = mybir.dt.uint32
+U8 = mybir.dt.uint8
+FP8X4 = mybir.dt.float8_e4m3fn_x4
+FP4X4 = mybir.dt.float4_e2m1fn_x4
+ADD = mybir.AluOpType.add
+MAX = mybir.AluOpType.max
+MIN = mybir.AluOpType.min
+MULT = mybir.AluOpType.mult
+EXP = mybir.ActivationFunctionType.Exp
+RELU = mybir.ActivationFunctionType.Relu
+
+P = 128
+PACK = 4
+IMAGES = 4
+SIDE = 64
+PASSES = 2
+PASS_CHANNELS = 64
+HID = 128
+
+CHUNK_ROWS = 16
+CHUNK = CHUNK_ROWS * SIDE
+CHUNKS_PER_IMAGE = SIDE // CHUNK_ROWS
+N_CHUNKS = IMAGES * CHUNKS_PER_IMAGE
+BANK = 512
+BANKS_PER_CHUNK = CHUNK // BANK
+PITCH = SIDE + 1
+BANK_ROWS = BANK // SIDE
+
+PATCH_ROWS = 8
+PATCH_COLS = 16
+TENSOR_ROWS = PATCH_ROWS - 2
+STRIPS = 5
+STRIP_STEP = 12
+VECTOR_ROWS = BANK_ROWS - TENSOR_ROWS
+BANKS_PER_IMAGE = SIDE // BANK_ROWS
+VECTOR_PIXELS = VECTOR_ROWS * SIDE
+TENSOR_PIXELS = TENSOR_ROWS * SIDE
+PAD_ROWS = SIDE + BANK_ROWS
+
+QUANTISE_LAG = 4
+FINISH_LAG = 5
+
+
+def tile_qca_operator_deep_pa_t_kernel(tc, x_cat, w1_words, w1_scales, out):
+    nc = tc.nc
+    with ExitStack() as stack:
+        keep = stack.enter_context(tc.tile_pool(name="keep", bufs=1))
+        sums = stack.enter_context(tc.tile_pool(name="sums", bufs=2))
+        nbrs = stack.enter_context(tc.tile_pool(name="nbrs", bufs=5))
+        strip_pool = stack.enter_context(tc.tile_pool(name="strip_pool", bufs=2))
+        patches = stack.enter_context(tc.tile_pool(name="patches", bufs=2 * BANKS_PER_CHUNK))
+        moving = stack.enter_context(tc.tile_pool(name="moving", bufs=(QUANTISE_LAG + 2) * BANKS_PER_CHUNK))
+        packed = stack.enter_context(tc.tile_pool(name="packed", bufs=3))
+        tails = stack.enter_context(tc.tile_pool(name="tails", bufs=FINISH_LAG - QUANTISE_LAG + 1))
+        results = stack.enter_context(tc.tile_pool(name="results", bufs=8))
+        psum_flip = stack.enter_context(tc.psum_pool(name="psum_flip", bufs=BANKS_PER_CHUNK))
+        psum_nbr = stack.enter_context(tc.psum_pool(name="psum_nbr", bufs=BANKS_PER_CHUNK))
+        psum_acc = stack.enter_context(tc.psum_pool(name="psum_acc", bufs=2 * BANKS_PER_CHUNK))
+
+        x_pad = keep.tile([P, IMAGES, PAD_ROWS, SIDE], BF16, name="x_pad")
+        nc.vector.memset(x_pad[:, :, 0 : SIDE + 2 : SIDE + 1, :], 0.0)
+        col_sum = {}
+        for banks in (BANKS_PER_CHUNK, BANKS_PER_IMAGE):
+            col_sum[banks] = keep.tile([P, banks * VECTOR_ROWS * PITCH + 2], F32, name="col_sum%d" % banks)
+            nc.vector.memset(col_sum[banks][:], 0.0)
+        w_codes = keep.tile([P, PASSES, 2 * HID], U8, name="w_codes", align_bytes=64)
+        w_planes = keep.tile([P, PASSES, HID], U8, name="w_planes", align_bytes=64)
+        nc.vector.memset(w_planes[:].rearrange("p g n -> p (g n)").bitcast(I32), 0)
+
+        def load_rows(b, first, count):
+            for g in range(PASSES):
+                nc.sync.dma_start(
+                    out=x_pad[g::PASSES, b, 1 + first : 1 + first + count, :].rearrange("c i j -> c (i j)"),
+                    in_=x_cat[b, g * PASS_CHANNELS : (g + 1) * PASS_CHANNELS, first : first + count, :].rearrange(
+                        "c i j -> c (i j)"
+                    ),
+                )
+
+        for part in range(CHUNKS_PER_IMAGE):
+            load_rows(0, part * CHUNK_ROWS, CHUNK_ROWS)
+        for g in range(PASSES):
+            nc.sync.dma_start(out=w_codes[:, g, :].bitcast(I32), in_=w1_words[g].bitcast(I32))
+            for quadrant in range(4):
+                nc.sync.dma_start(
+                    out=w_planes[32 * quadrant : 32 * quadrant + 4, g, :].bitcast(I32),
+                    in_=w1_scales[g, 4 * quadrant : 4 * quadrant + 4, :].bitcast(I32),
+                )
+        for b in range(1, IMAGES):
+            load_rows(b, 0, SIDE)
+
+        ident = keep.tile([P, P], BF16, name="ident")
+        make_identity(nc, ident[:])
+        ident_pad = keep.tile([P, PATCH_ROWS, PATCH_COLS + 2], BF16, name="ident_pad")
+        nc.vector.memset(ident_pad[:], 0.0)
+        nc.vector.tensor_copy(
+            out=ident_pad[:, :, 1 : PATCH_COLS + 1], in_=ident[:].rearrange("p (i j) -> p i j", j=PATCH_COLS)
+        )
+        beside = keep.tile([P, PATCH_ROWS, PATCH_COLS], BF16, name="beside")
+        nc.vector.tensor_tensor(
+            out=beside[:], in0=ident_pad[:, :, 0:PATCH_COLS], in1=ident_pad[:, :, 2 : PATCH_COLS + 2], op=ADD
+        )
+        around = keep.tile([P, PATCH_ROWS, PATCH_COLS], BF16, name="around")
+        nc.vector.tensor_tensor(out=around[:], in0=beside[:], in1=ident_pad[:, :, 1 : PATCH_COLS + 1], op=ADD)
+        outer = keep.tile([P, TENSOR_ROWS, PATCH_COLS], BF16, name="outer")
+        nc.vector.tensor_tensor(
+            out=outer[:], in0=around[:, 0:TENSOR_ROWS, :], in1=around[:, 2 : TENSOR_ROWS + 2, :], op=ADD
+        )
+        window = keep.tile([P, TENSOR_ROWS, PATCH_COLS], BF16, name="window")
+        nc.vector.tensor_tensor(out=window[:], in0=outer[:], in1=beside[:, 1 : TENSOR_ROWS + 1, :], op=ADD)
+
+        above_below = {}
+        left_right = {}
+        nbr = {}
+        strips = {}
+        flipped = {}
+        nbr_acc = {}
+        xn = {}
+        acc = {}
+        neg = {}
+
+        def rows_of(flat):
+            return flat.rearrange("p (g r j) -> p g r j", r=VECTOR_ROWS, j=SIDE)
+
+        def column_sums(batch, shift):
+            banks = batch[2]
+            return col_sum[banks][:, shift : shift + banks * VECTOR_ROWS * PITCH].rearrange(
+                "p (g r j) -> p g r j", r=VECTOR_ROWS, j=PITCH
+            )[:, :, :, 0:SIDE]
+
+        def padded_rows(batch, offset):
+            b, first, banks = batch
+            top = first * BANK_ROWS + TENSOR_ROWS + offset
+            return x_pad[:, b, top : top + banks * BANK_ROWS, :].rearrange("p (g r) j -> p g r j", r=BANK_ROWS)[
+                :, :, 0:VECTOR_ROWS, :
+            ]
+
+        def add_above_and_below(batch):
+            above_below[batch] = sums.tile([P, batch[2] * VECTOR_PIXELS], F32, name="above_below")
+            nc.vector.tensor_tensor(
+                out=rows_of(above_below[batch][:]), in0=padded_rows(batch, 0), in1=padded_rows(batch, 2), op=ADD
+            )
+
+        def add_centre(batch):
+            nc.vector.tensor_tensor(
+                out=column_sums(batch, 1), in0=rows_of(above_below[batch][:]), in1=padded_rows(batch, 1), op=ADD
+            )
+
+        def add_left_and_right(batch):
+            left_right[batch] = sums.tile([P, batch[2] * VECTOR_PIXELS], F32, name="left_right")
+            nc.vector.tensor_tensor(
+                out=rows_of(left_right[batch][:]), in0=column_sums(batch, 0), in1=column_sums(batch, 2), op=ADD
+            )
+
+        def add_up_and_round(batch):
+            b, first, banks = batch
+            rounded = nbrs.tile([P, banks * VECTOR_PIXELS], BF16, name="rounded")
+            nc.vector.tensor_tensor(out=rounded[:], in0=left_right[batch][:], in1=above_below[batch][:], op=ADD)
+            for g in range(banks):
+                nbr[b, first + g] = rounded[:, g * VECTOR_PIXELS : (g + 1) * VECTOR_PIXELS]
+
+        add_steps = [add_above_and_below, add_centre, add_left_and_right, add_up_and_round]
+
+        def copy_strip(b, s, first, count):
+            if b not in strips:
+                strips[b] = strip_pool.tile([P, STRIPS, SIDE, PATCH_COLS], BF16, name="strips")
+            nc.vector.tensor_copy(
+                out=strips[b][:, s, first : first + count, :],
+                in_=x_pad[:, b, first : first + count, s * STRIP_STEP : s * STRIP_STEP + PATCH_COLS],
+            )
+
+        def transpose_patches(k):
+            b, part = divmod(k, CHUNKS_PER_IMAGE)
+            for h in range(BANKS_PER_CHUNK):
+                flipped[k, h] = psum_flip.tile([P, STRIPS, P], BF16, name="flipped")
+                first = part * CHUNK_ROWS + h * BANK_ROWS
+                for s in range(STRIPS):
+                    nc.tensor.transpose(
+                        flipped[k, h][:, s, :],
+                        strips[b][:, s, first : first + PATCH_ROWS, :].rearrange("p i j -> p (i j)"),
+                        ident[:],
+                    )
+
+        def sum_on_tensor_engine(k, h):
+            blocks = patches.tile([P, STRIPS, P], BF16, name="blocks")
+            nc.vector.tensor_copy(out=blocks[:], in_=flipped[k, h][:])
+            nbr_acc[k, h] = psum_nbr.tile([P, TENSOR_ROWS, SIDE], F32, name="nbr_acc")
+            for s in range(STRIPS):
+                lo = 0 if s == 0 else 1
+                hi = PATCH_COLS if s == STRIPS - 1 else STRIP_STEP + 1
+                nc.tensor.matmul(
+                    out=nbr_acc[k, h][:, :, s * STRIP_STEP + lo : s * STRIP_STEP + hi],
+                    lhsT=blocks[:, s, :],
+                    rhs=window[:, :, lo:hi],
+                    start=True,
+                    stop=True,
+                )
+
+        def spread_second_pass(k, h):
+            nc.sync.dma_start(
+                out=xn[k, h][:, BANK * PACK : PASSES * BANK * PACK],
+                in_=xn[k, h][1::PASSES, 0 : BANK * PACK].unsqueeze(1).to_broadcast([PASS_CHANNELS, 2, BANK * PACK]),
+            )
+
+        def spread_first_pass(k, h):
+            nc.sync.dma_start(out=xn[k, h][1::PASSES, 0 : BANK * PACK], in_=xn[k, h][0::PASSES, 0 : BANK * PACK])
+
+        def repeat_tensor_rows(k, h):
+            xn[k, h] = moving.tile([P, PASSES * BANK * PACK], BF16, name="xn", align_bytes=64)
+            nc.scalar.copy(
+                out=xn[k, h][:, 0 : TENSOR_PIXELS * PACK].rearrange("p (w t) -> p w t", t=PACK),
+                in_=nbr_acc[k, h][:]
+                .rearrange("p o j -> p (o j)")
+                .unsqueeze(2)
+                .to_broadcast([P, TENSOR_PIXELS, PACK]),
+            )
+
+        def repeat_vector_rows(k, h):
+            copy = nc.vector.tensor_copy if k < QUANTISE_LAG else nc.scalar.copy
+            copy(
+                out=xn[k, h][:, TENSOR_PIXELS * PACK : BANK * PACK].rearrange("p (w t) -> p w t", t=PACK),
+                in_=nbr[k // CHUNKS_PER_IMAGE, (k % CHUNKS_PER_IMAGE) * BANKS_PER_CHUNK + h]
+                .unsqueeze(2)
+                .to_broadcast([P, VECTOR_PIXELS, PACK]),
+            )
+            spread_second_pass(k, h)
+
+        def quantise_and_multiply(k, h):
+            codes = packed.tile([P, PASSES * BANK], U32, name="codes", align_bytes=64)
+            planes = packed.tile([P, PASSES * BANK], U8, name="planes", align_bytes=64)
+            nc.vector.quantize_mx(out=codes[:].bitcast(FP8X4), scales=planes[:], in_=xn[k, h][:])
+            acc[k, h] = psum_acc.tile([HID, BANK], F32, name="acc")
+            for g in range(PASSES):
+                nc.tensor.matmul_mx(
+                    out=acc[k, h][:],
+                    lhsT=w_codes[:, g, :].bitcast(FP4X4),
+                    lhsT_scale=w_planes[:, g, :],
+                    rhs=codes[:, g * BANK : (g + 1) * BANK].bitcast(FP8X4),
+                    rhs_scale=planes[:, g * BANK : (g + 1) * BANK],
+                    start=(g == 0),
+                    stop=(g == PASSES - 1),
+                )
+
+        def scalar_takes(k, h):
+            return k >= N_CHUNKS - QUANTISE_LAG
+
+        def exponentials(k):
+            neg[k] = tails.tile([HID, CHUNK], F32, name="neg")
+            for h in range(BANKS_PER_CHUNK):
+                nc.scalar.activation(out=neg[k][:, h * BANK : (h + 1) * BANK], in_=acc[k, h][:], func=EXP)
+
+        def negative_part(k, on_scalar):
+            mine = [h for h in range(BANKS_PER_CHUNK) if scalar_takes(k, h) == on_scalar]
+            if on_scalar:
+                for h in mine:
+                    part = neg[k][:, h * BANK : (h + 1) * BANK]
+                    nc.scalar.activation(out=part, in_=part, func=RELU, bias=1.0, scale=-1.0)
+            elif mine:
+                part = neg[k][:, mine[0] * BANK : (mine[-1] + 1) * BANK]
+                nc.vector.tensor_scalar(out=part, in0=part, scalar1=1.0, scalar2=-1.0, op0=MIN, op1=ADD)
+
+        def finish(k, h):
+            res = results.tile([HID, BANK], F32, name="res")
+            nc.vector.scalar_tensor_tensor(
+                out=res[:],
+                in0=neg[k][:, h * BANK : (h + 1) * BANK],
+                scalar=-1.0 if scalar_takes(k, h) else 1.0,
+                in1=acc[k, h][:],
+                op0=MULT,
+                op1=MAX,
+            )
+            b, part = divmod(k, CHUNKS_PER_IMAGE)
+            bank_rows = BANK // SIDE
+            first = part * CHUNK_ROWS + h * bank_rows
+            nc.sync.dma_start(out=out[b, :, first : first + bank_rows, :].rearrange("o i j -> o (i j)"), in_=res[:])
+
+        def whole_sums(j):
+            if j < 2:
+                return [(0, (2 * j + i) * BANKS_PER_CHUNK, BANKS_PER_CHUNK) for i in range(2)]
+            return []
+
+        def single_adds(j):
+            if j in (2, 3):
+                first = 2 * (j - 2)
+                return [(0, (add_steps[first], (1, 0, BANKS_PER_IMAGE))), (2, (add_steps[first + 1], (1, 0, BANKS_PER_IMAGE)))]
+            b, stage = divmod(j + CHUNKS_PER_IMAGE, CHUNKS_PER_IMAGE)
+            if 2 <= b < IMAGES:
+                return [(1, (add_steps[stage], (b, 0, BANKS_PER_IMAGE)))]
+            return []
+
+        with tc.manual_schedule():
+            for s in range(STRIPS):
+                copy_strip(0, s, 0, CHUNK_ROWS)
+            transpose_patches(0)
+            for j in range(N_CHUNKS + FINISH_LAG):
+                repeating = j < N_CHUNKS
+                q = j - QUANTISE_LAG
+                quantising = 0 <= q < N_CHUNKS
+                f = j - FINISH_LAG
+                finishing = 0 <= f
+                summed = whole_sums(j)
+                singles = single_adds(j)
+                for batch in summed:
+                    add_above_and_below(batch)
+                for place, (step, batch) in singles:
+                    if place == 0:
+                        step(batch)
+                if quantising:
+                    quantise_and_multiply(q, 0)
+                if finishing:
+                    negative_part(f, False)
+                for batch in summed[0:1]:
+                    add_centre(batch)
+                for place, (step, batch) in singles:
+                    if place == 1:
+                        step(batch)
+                if quantising:
+                    quantise_and_multiply(q, 1)
+                    exponentials(q)
+                    negative_part(q, True)
+                for batch in summed[0:1]:
+                    add_left_and_right(batch)
+                if repeating:
+                    for h in range(BANKS_PER_CHUNK):
+                        sum_on_tensor_engine(j, h)
+                        repeat_tensor_rows(j, h)
+                if finishing:
+                    finish(f, 0)
+                    finish(f, 1)
+                for batch in summed[0:1]:
+                    add_up_and_round(batch)
+                for batch in summed[1:2]:
+                    add_centre(batch)
+                for place, (step, batch) in singles:
+                    if place == 2:
+                        step(batch)
+                if repeating:
+                    repeat_vector_rows(j, 0)
+                for batch in summed[1:2]:
+                    add_left_and_right(batch)
+                if repeating:
+                    repeat_vector_rows(j, 1)
+                    for h in range(BANKS_PER_CHUNK):
+                        spread_first_pass(j, h)
+                for batch in summed[1:2]:
+                    add_up_and_round(batch)
+                if j == 0:
+                    for s in range(STRIPS):
+                        copy_strip(0, s, CHUNK_ROWS, SIDE - CHUNK_ROWS)
+                b, part = divmod(j, CHUNKS_PER_IMAGE)
+                if b + 1 < IMAGES:
+                    for s in range(STRIPS):
+                        if min(s, CHUNKS_PER_IMAGE - 1) == part:
+                            copy_strip(b + 1, s, 0, SIDE)
+                if j + 1 < N_CHUNKS:
+                    transpose_patches(j + 1)

@@ -23,8 +23,9 @@ P = 128
 PACK = 4
 IMAGES = 4
 SIDE = 64
-PASSES = 2
-PASS_CHANNELS = 64
+WORDS = 2
+HALVES = 2
+GROUPS = 2
 HID = 128
 
 CHUNK_ROWS = 16
@@ -35,7 +36,6 @@ BANK = 512
 BANKS_PER_CHUNK = CHUNK // BANK
 PITCH = SIDE + 1
 BANK_ROWS = BANK // SIDE
-
 PATCH_ROWS = 8
 PATCH_COLS = 16
 TENSOR_ROWS = PATCH_ROWS - 2
@@ -47,59 +47,64 @@ VECTOR_PIXELS = VECTOR_ROWS * SIDE
 TENSOR_PIXELS = TENSOR_ROWS * SIDE
 PAD_ROWS = SIDE + BANK_ROWS
 
-QUANTISE_LAG = 4
-FINISH_LAG = 5
-
 
 def tile_qca_operator_deep_pa_t_kernel(tc, x_cat, w1_words, w1_scales, out):
     nc = tc.nc
     with ExitStack() as stack:
         keep = stack.enter_context(tc.tile_pool(name="keep", bufs=1))
         sums = stack.enter_context(tc.tile_pool(name="sums", bufs=2))
-        nbrs = stack.enter_context(tc.tile_pool(name="nbrs", bufs=5))
+        nbrs = stack.enter_context(tc.tile_pool(name="nbrs", bufs=4))
         strip_pool = stack.enter_context(tc.tile_pool(name="strip_pool", bufs=2))
-        patches = stack.enter_context(tc.tile_pool(name="patches", bufs=2 * BANKS_PER_CHUNK))
-        moving = stack.enter_context(tc.tile_pool(name="moving", bufs=(QUANTISE_LAG + 2) * BANKS_PER_CHUNK))
-        packed = stack.enter_context(tc.tile_pool(name="packed", bufs=3))
-        tails = stack.enter_context(tc.tile_pool(name="tails", bufs=FINISH_LAG - QUANTISE_LAG + 1))
+        patches = stack.enter_context(tc.tile_pool(name="patches", bufs=4))
+        moving = stack.enter_context(tc.tile_pool(name="moving", bufs=8))
+        packed = stack.enter_context(tc.tile_pool(name="packed", bufs=4))
+        tails = stack.enter_context(tc.tile_pool(name="tails", bufs=3))
         results = stack.enter_context(tc.tile_pool(name="results", bufs=8))
-        psum_flip = stack.enter_context(tc.psum_pool(name="psum_flip", bufs=BANKS_PER_CHUNK))
-        psum_nbr = stack.enter_context(tc.psum_pool(name="psum_nbr", bufs=BANKS_PER_CHUNK))
-        psum_acc = stack.enter_context(tc.psum_pool(name="psum_acc", bufs=2 * BANKS_PER_CHUNK))
+        psum_flip = stack.enter_context(tc.psum_pool(name="psum_flip", bufs=2))
+        psum_nbr = stack.enter_context(tc.psum_pool(name="psum_nbr", bufs=2))
+        psum_acc = stack.enter_context(tc.psum_pool(name="psum_acc", bufs=4))
 
         x_pad = keep.tile([P, IMAGES, PAD_ROWS, SIDE], BF16, name="x_pad")
-        nc.vector.memset(x_pad[:, :, 0 : SIDE + 2 : SIDE + 1, :], 0.0)
-        col_sum = {}
-        for banks in (BANKS_PER_CHUNK, BANKS_PER_IMAGE):
-            col_sum[banks] = keep.tile([P, banks * VECTOR_ROWS * PITCH + 2], F32, name="col_sum%d" % banks)
-            nc.vector.memset(col_sum[banks][:], 0.0)
-        w_codes = keep.tile([P, PASSES, 2 * HID], U8, name="w_codes", align_bytes=64)
-        w_planes = keep.tile([P, PASSES, HID], U8, name="w_planes", align_bytes=64)
-        nc.vector.memset(w_planes[:].rearrange("p g n -> p (g n)").bitcast(I32), 0)
+        nc.gpsimd.memset(x_pad[:, :, 0 : SIDE + 2 : SIDE + 1, :], 0.0)
+        w_codes = keep.tile([P, WORDS, HALVES, 2 * HID], U8, name="w_codes", align_bytes=64)
+        w_planes = keep.tile([P, HALVES, HID], U8, name="w_planes", align_bytes=64)
+        ident = keep.tile([P, P], BF16, name="ident")
+        make_identity(nc, ident[:])
+        nc.gpsimd.memset(w_codes[:].rearrange("p h d n -> p (h d n)").bitcast(I32), 0)
+        nc.gpsimd.memset(w_planes[:].rearrange("p d n -> p (d n)").bitcast(I32), 0)
 
         def load_rows(b, first, count):
-            for g in range(PASSES):
+            for d in range(HALVES):
                 nc.sync.dma_start(
-                    out=x_pad[g::PASSES, b, 1 + first : 1 + first + count, :].rearrange("c i j -> c (i j)"),
-                    in_=x_cat[b, g * PASS_CHANNELS : (g + 1) * PASS_CHANNELS, first : first + count, :].rearrange(
-                        "c i j -> c (i j)"
-                    ),
+                    out=x_pad[d::HALVES, b, 1 + first : 1 + first + count, :].rearrange("c i j -> c (i j)"),
+                    in_=x_cat[b, :, first : first + count, :].rearrange(
+                        "(g d m) i j -> d g m (i j)", g=GROUPS, d=HALVES
+                    )[d],
                 )
 
         for part in range(CHUNKS_PER_IMAGE):
             load_rows(0, part * CHUNK_ROWS, CHUNK_ROWS)
-        for g in range(PASSES):
-            nc.sync.dma_start(out=w_codes[:, g, :].bitcast(I32), in_=w1_words[g].bitcast(I32))
-            for quadrant in range(4):
+        for g in range(GROUPS):
+            for d in range(HALVES):
                 nc.sync.dma_start(
-                    out=w_planes[32 * quadrant : 32 * quadrant + 4, g, :].bitcast(I32),
-                    in_=w1_scales[g, 4 * quadrant : 4 * quadrant + 4, :].bitcast(I32),
+                    out=w_codes[64 * g + d : 64 * (g + 1) : 2, :, d, :].bitcast(I32),
+                    in_=w1_words[g, 64 * d : 64 * (d + 1), :].rearrange("(m h) n -> m h n", h=WORDS).bitcast(I32),
+                )
+        for d in range(HALVES):
+            for quadrant in range(4):
+                g, first = divmod(quadrant, 2)
+                row = 8 * d + 4 * first
+                nc.sync.dma_start(
+                    out=w_planes[32 * quadrant : 32 * quadrant + 4, d, :].bitcast(I32),
+                    in_=w1_scales[g, row : row + 4, :].bitcast(I32),
                 )
         for b in range(1, IMAGES):
             load_rows(b, 0, SIDE)
 
-        ident = keep.tile([P, P], BF16, name="ident")
-        make_identity(nc, ident[:])
+        col_sum = {}
+        for banks in (2, 6, 8):
+            col_sum[banks] = keep.tile([P, banks * VECTOR_ROWS * PITCH + 2], F32, name="col_sum%d" % banks)
+            nc.gpsimd.memset(col_sum[banks][:, 0 : banks * VECTOR_ROWS * PITCH + 1 : PITCH], 0.0)
         ident_pad = keep.tile([P, PATCH_ROWS, PATCH_COLS + 2], BF16, name="ident_pad")
         nc.vector.memset(ident_pad[:], 0.0)
         nc.vector.tensor_copy(
@@ -178,188 +183,205 @@ def tile_qca_operator_deep_pa_t_kernel(tc, x_cat, w1_words, w1_scales, out):
                 in_=x_pad[:, b, first : first + count, s * STRIP_STEP : s * STRIP_STEP + PATCH_COLS],
             )
 
-        def transpose_patches(k):
-            b, part = divmod(k, CHUNKS_PER_IMAGE)
-            for h in range(BANKS_PER_CHUNK):
-                flipped[k, h] = psum_flip.tile([P, STRIPS, P], BF16, name="flipped")
-                first = part * CHUNK_ROWS + h * BANK_ROWS
-                for s in range(STRIPS):
-                    nc.tensor.transpose(
-                        flipped[k, h][:, s, :],
-                        strips[b][:, s, first : first + PATCH_ROWS, :].rearrange("p i j -> p (i j)"),
-                        ident[:],
-                    )
+        def transpose_patches(n):
+            b, g = divmod(n, BANKS_PER_IMAGE)
+            flipped[n] = psum_flip.tile([P, STRIPS, P], BF16, name="flipped")
+            for s in range(STRIPS):
+                nc.tensor.transpose(
+                    flipped[n][:, s, :],
+                    strips[b][:, s, g * BANK_ROWS : g * BANK_ROWS + PATCH_ROWS, :].rearrange("p i j -> p (i j)"),
+                    ident[:],
+                )
 
-        def sum_on_tensor_engine(k, h):
-            blocks = patches.tile([P, STRIPS, P], BF16, name="blocks")
-            nc.vector.tensor_copy(out=blocks[:], in_=flipped[k, h][:])
-            nbr_acc[k, h] = psum_nbr.tile([P, TENSOR_ROWS, SIDE], F32, name="nbr_acc")
+        blocks_of = {}
+
+        def patches_on_scalar(n):
+            return False
+
+        def repeats_on_vector(n):
+            return False
+
+        def copy_patches(n):
+            blocks_of[n] = patches.tile([P, STRIPS, P], BF16, name="blocks")
+            copy = nc.scalar.copy if patches_on_scalar(n) else nc.vector.tensor_copy
+            copy(out=blocks_of[n][:], in_=flipped[n][:])
+
+        def sum_on_tensor_engine(n):
+            blocks = blocks_of[n]
+            nbr_acc[n] = psum_nbr.tile([P, TENSOR_ROWS, SIDE], F32, name="nbr_acc")
             for s in range(STRIPS):
                 lo = 0 if s == 0 else 1
                 hi = PATCH_COLS if s == STRIPS - 1 else STRIP_STEP + 1
                 nc.tensor.matmul(
-                    out=nbr_acc[k, h][:, :, s * STRIP_STEP + lo : s * STRIP_STEP + hi],
+                    out=nbr_acc[n][:, :, s * STRIP_STEP + lo : s * STRIP_STEP + hi],
                     lhsT=blocks[:, s, :],
                     rhs=window[:, :, lo:hi],
                     start=True,
                     stop=True,
                 )
 
-        def spread_second_pass(k, h):
-            nc.sync.dma_start(
-                out=xn[k, h][:, BANK * PACK : PASSES * BANK * PACK],
-                in_=xn[k, h][1::PASSES, 0 : BANK * PACK].unsqueeze(1).to_broadcast([PASS_CHANNELS, 2, BANK * PACK]),
-            )
 
-        def spread_first_pass(k, h):
-            nc.sync.dma_start(out=xn[k, h][1::PASSES, 0 : BANK * PACK], in_=xn[k, h][0::PASSES, 0 : BANK * PACK])
+        def xn_tiles(n):
+            xn[n] = moving.tile([P, BANK * PACK], BF16, name="xn", align_bytes=64)
 
-        def repeat_tensor_rows(k, h):
-            xn[k, h] = moving.tile([P, PASSES * BANK * PACK], BF16, name="xn", align_bytes=64)
+        def repeat_tensor_rows(n):
             nc.scalar.copy(
-                out=xn[k, h][:, 0 : TENSOR_PIXELS * PACK].rearrange("p (w t) -> p w t", t=PACK),
-                in_=nbr_acc[k, h][:]
+                out=xn[n][:, 0 : TENSOR_PIXELS * PACK].rearrange("p (w t) -> p w t", t=PACK),
+                in_=nbr_acc[n][:]
                 .rearrange("p o j -> p (o j)")
                 .unsqueeze(2)
                 .to_broadcast([P, TENSOR_PIXELS, PACK]),
             )
 
-        def repeat_vector_rows(k, h):
-            copy = nc.vector.tensor_copy if k < QUANTISE_LAG else nc.scalar.copy
+        def repeat_vector_rows(n):
+            copy = nc.vector.tensor_copy if repeats_on_vector(n) else nc.scalar.copy
             copy(
-                out=xn[k, h][:, TENSOR_PIXELS * PACK : BANK * PACK].rearrange("p (w t) -> p w t", t=PACK),
-                in_=nbr[k // CHUNKS_PER_IMAGE, (k % CHUNKS_PER_IMAGE) * BANKS_PER_CHUNK + h]
+                out=xn[n][:, TENSOR_PIXELS * PACK : BANK * PACK].rearrange("p (w t) -> p w t", t=PACK),
+                in_=nbr[divmod(n, BANKS_PER_IMAGE)]
                 .unsqueeze(2)
                 .to_broadcast([P, VECTOR_PIXELS, PACK]),
             )
-            spread_second_pass(k, h)
 
-        def quantise_and_multiply(k, h):
-            codes = packed.tile([P, PASSES * BANK], U32, name="codes", align_bytes=64)
-            planes = packed.tile([P, PASSES * BANK], U8, name="planes", align_bytes=64)
-            nc.vector.quantize_mx(out=codes[:].bitcast(FP8X4), scales=planes[:], in_=xn[k, h][:])
-            acc[k, h] = psum_acc.tile([HID, BANK], F32, name="acc")
-            for g in range(PASSES):
+        codes = {}
+        planes = {}
+
+        def quantise(n, w):
+            if w == 0:
+                codes[n] = packed.tile([P, WORDS * BANK], U32, name="codes", align_bytes=64)
+                planes[n] = packed.tile([P, WORDS * BANK], U8, name="planes", align_bytes=64)
+            part = slice(w * BANK, (w + 1) * BANK)
+            nc.vector.quantize_mx(out=codes[n][:, part].bitcast(FP8X4), scales=planes[n][:, part], in_=xn[n][:])
+
+        def multiply(n, w):
+            if w == 0:
+                acc[n] = psum_acc.tile([HID, BANK], F32, name="acc")
+            part = slice(w * BANK, (w + 1) * BANK)
+            for d in range(HALVES):
                 nc.tensor.matmul_mx(
-                    out=acc[k, h][:],
-                    lhsT=w_codes[:, g, :].bitcast(FP4X4),
-                    lhsT_scale=w_planes[:, g, :],
-                    rhs=codes[:, g * BANK : (g + 1) * BANK].bitcast(FP8X4),
-                    rhs_scale=planes[:, g * BANK : (g + 1) * BANK],
-                    start=(g == 0),
-                    stop=(g == PASSES - 1),
+                    out=acc[n][:],
+                    lhsT=w_codes[:, w, d, :].bitcast(FP4X4),
+                    lhsT_scale=w_planes[:, d, :],
+                    rhs=codes[n][:, part].bitcast(FP8X4),
+                    rhs_scale=planes[n][:, part],
+                    start=(w == 0 and d == 0),
+                    stop=(w == WORDS - 1 and d == HALVES - 1),
                 )
 
-        def scalar_takes(k, h):
-            return k >= N_CHUNKS - QUANTISE_LAG
+        one = {}
 
-        def exponentials(k):
-            neg[k] = tails.tile([HID, CHUNK], F32, name="neg")
-            for h in range(BANKS_PER_CHUNK):
-                nc.scalar.activation(out=neg[k][:, h * BANK : (h + 1) * BANK], in_=acc[k, h][:], func=EXP)
+        def exponential(k, h):
+            if h == 0:
+                neg[k] = tails.tile([HID, CHUNK], F32, name="neg")
+            nc.scalar.activation(out=neg[k][:, h * BANK : (h + 1) * BANK], in_=acc[2 * k + h][:], func=EXP)
 
-        def negative_part(k, on_scalar):
-            mine = [h for h in range(BANKS_PER_CHUNK) if scalar_takes(k, h) == on_scalar]
-            if on_scalar:
-                for h in mine:
-                    part = neg[k][:, h * BANK : (h + 1) * BANK]
-                    nc.scalar.activation(out=part, in_=part, func=RELU, bias=1.0, scale=-1.0)
-            elif mine:
-                part = neg[k][:, mine[0] * BANK : (mine[-1] + 1) * BANK]
-                nc.vector.tensor_scalar(out=part, in0=part, scalar1=1.0, scalar2=-1.0, op0=MIN, op1=ADD)
+        def on_gpsimd(k):
+            return k < N_CHUNKS - 2
+
+        def release_gpsimd(k):
+            one[k] = tails.tile([P, 1], F32, name="one")
+            nc.vector.memset(one[k][:], 1.0)
+
+        def negative_part(k, h, scalar1=1.0, engine=nc.vector):
+            part = neg[k][:, h * BANK : (h + 1) * BANK]
+            engine.tensor_scalar(out=part, in0=part, scalar1=scalar1, scalar2=-1.0, op0=MIN, op1=ADD)
 
         def finish(k, h):
+            n = 2 * k + h
             res = results.tile([HID, BANK], F32, name="res")
-            nc.vector.scalar_tensor_tensor(
-                out=res[:],
-                in0=neg[k][:, h * BANK : (h + 1) * BANK],
-                scalar=-1.0 if scalar_takes(k, h) else 1.0,
-                in1=acc[k, h][:],
-                op0=MULT,
-                op1=MAX,
+            nc.vector.tensor_tensor(out=res[:], in0=acc[n][:], in1=neg[k][:, h * BANK : (h + 1) * BANK], op=MAX)
+            b, g = divmod(n, BANKS_PER_IMAGE)
+            nc.sync.dma_start(
+                out=out[b, :, g * BANK_ROWS : (g + 1) * BANK_ROWS, :].rearrange("o i j -> o (i j)"), in_=res[:]
             )
-            b, part = divmod(k, CHUNKS_PER_IMAGE)
-            bank_rows = BANK // SIDE
-            first = part * CHUNK_ROWS + h * bank_rows
-            nc.sync.dma_start(out=out[b, :, first : first + bank_rows, :].rearrange("o i j -> o (i j)"), in_=res[:])
 
-        def whole_sums(j):
-            if j < 2:
-                return [(0, (2 * j + i) * BANKS_PER_CHUNK, BANKS_PER_CHUNK) for i in range(2)]
-            return []
+        def xn_tile(n):
+            if n not in xn:
+                xn[n] = moving.tile([P, BANK * PACK], BF16, name="xn", align_bytes=64)
 
-        def single_adds(j):
-            if j in (2, 3):
-                first = 2 * (j - 2)
-                return [(0, (add_steps[first], (1, 0, BANKS_PER_IMAGE))), (2, (add_steps[first + 1], (1, 0, BANKS_PER_IMAGE)))]
-            b, stage = divmod(j + CHUNKS_PER_IMAGE, CHUNKS_PER_IMAGE)
-            if 2 <= b < IMAGES:
-                return [(1, (add_steps[stage], (b, 0, BANKS_PER_IMAGE)))]
-            return []
-
+        LAG = 2
         with tc.manual_schedule():
+            first_chunk = (0, 0, BANKS_PER_CHUNK)
+            rest = (0, BANKS_PER_CHUNK, BANKS_PER_IMAGE - BANKS_PER_CHUNK)
             for s in range(STRIPS):
                 copy_strip(0, s, 0, CHUNK_ROWS)
+                if s < 4:
+                    add_steps[s](first_chunk)
             transpose_patches(0)
-            for j in range(N_CHUNKS + FINISH_LAG):
-                repeating = j < N_CHUNKS
-                q = j - QUANTISE_LAG
+            transpose_patches(1)
+            for n in range(2):
+                xn_tile(n)
+                repeat_vector_rows(n)
+            copy_patches(0)
+            sum_on_tensor_engine(0)
+            copy_patches(1)
+            sum_on_tensor_engine(1)
+            for s in range(STRIPS):
+                copy_strip(0, s, CHUNK_ROWS, SIDE - CHUNK_ROWS)
+            transpose_patches(2)
+            transpose_patches(3)
+            add_steps[0](rest)
+            for c in range(N_CHUNKS + LAG + 1):
+                q = c - LAG
+                f = q - 1
+                summing = c < N_CHUNKS
+                ahead = c + 1 < N_CHUNKS
                 quantising = 0 <= q < N_CHUNKS
-                f = j - FINISH_LAG
                 finishing = 0 <= f
-                summed = whole_sums(j)
-                singles = single_adds(j)
-                for batch in summed:
-                    add_above_and_below(batch)
-                for place, (step, batch) in singles:
-                    if place == 0:
-                        step(batch)
-                if quantising:
-                    quantise_and_multiply(q, 0)
                 if finishing:
-                    negative_part(f, False)
-                for batch in summed[0:1]:
-                    add_centre(batch)
-                for place, (step, batch) in singles:
-                    if place == 1:
-                        step(batch)
+                    exponential(f, 0)
+                    exponential(f, 1)
+                if summing:
+                    for h in range(2):
+                        n = 2 * c + h
+                        xn_tile(n)
+                        repeat_tensor_rows(n)
+                        if c > 0 and not repeats_on_vector(n):
+                            repeat_vector_rows(n)
+                g_neg = finishing and on_gpsimd(f)
                 if quantising:
-                    quantise_and_multiply(q, 1)
-                    exponentials(q)
-                    negative_part(q, True)
-                for batch in summed[0:1]:
-                    add_left_and_right(batch)
-                if repeating:
-                    for h in range(BANKS_PER_CHUNK):
-                        sum_on_tensor_engine(j, h)
-                        repeat_tensor_rows(j, h)
+                    quantise(2 * q, 0)
+                    multiply(2 * q, 0)
+                    quantise(2 * q, 1)
+                    multiply(2 * q, 1)
+                    quantise(2 * q + 1, 0)
+                    multiply(2 * q + 1, 0)
+                if g_neg:
+                    release_gpsimd(f)
+                    negative_part(f, 0, one[f][:], nc.gpsimd)
+                    negative_part(f, 1, one[f][:], nc.gpsimd)
+                if finishing and not g_neg:
+                    negative_part(f, 0)
+                if quantising:
+                    quantise(2 * q + 1, 1)
+                    multiply(2 * q + 1, 1)
+                if ahead:
+                    copy_patches(2 * c + 2)
+                    sum_on_tensor_engine(2 * c + 2)
+                if c == 0:
+                    add_steps[1](rest)
+                if ahead:
+                    copy_patches(2 * c + 3)
+                if finishing and not g_neg:
+                    negative_part(f, 1)
+                if c + 2 < N_CHUNKS:
+                    transpose_patches(2 * c + 4)
+                    transpose_patches(2 * c + 5)
+                if ahead:
+                    sum_on_tensor_engine(2 * c + 3)
+                if summing:
+                    for h in range(2):
+                        n = 2 * c + h
+                        if c > 0 and repeats_on_vector(n):
+                            repeat_vector_rows(n)
                 if finishing:
                     finish(f, 0)
                     finish(f, 1)
-                for batch in summed[0:1]:
-                    add_up_and_round(batch)
-                for batch in summed[1:2]:
-                    add_centre(batch)
-                for place, (step, batch) in singles:
-                    if place == 2:
-                        step(batch)
-                if repeating:
-                    repeat_vector_rows(j, 0)
-                for batch in summed[1:2]:
-                    add_left_and_right(batch)
-                if repeating:
-                    repeat_vector_rows(j, 1)
-                    for h in range(BANKS_PER_CHUNK):
-                        spread_first_pass(j, h)
-                for batch in summed[1:2]:
-                    add_up_and_round(batch)
-                if j == 0:
-                    for s in range(STRIPS):
-                        copy_strip(0, s, CHUNK_ROWS, SIDE - CHUNK_ROWS)
-                b, part = divmod(j, CHUNKS_PER_IMAGE)
+                if c == 0:
+                    add_steps[2](rest)
+                    add_steps[3](rest)
+                b, part = divmod(c, CHUNKS_PER_IMAGE)
                 if b + 1 < IMAGES:
-                    for s in range(STRIPS):
-                        if min(s, CHUNKS_PER_IMAGE - 1) == part:
+                    add_steps[part]((b + 1, 0, BANKS_PER_IMAGE))
+                    if part < 2:
+                        for s in range(3 * part, min(3 * part + 3, STRIPS)):
                             copy_strip(b + 1, s, 0, SIDE)
-                if j + 1 < N_CHUNKS:
-                    transpose_patches(j + 1)

@@ -38,14 +38,12 @@ PITCH = SIDE + 1
 BANK_ROWS = BANK // SIDE
 PATCH_ROWS = 8
 PATCH_COLS = 16
-TENSOR_ROWS = PATCH_ROWS - 2
 STRIPS = 5
 STRIP_STEP = 12
-VECTOR_ROWS = BANK_ROWS - TENSOR_ROWS
+PAIR = 2
 BANKS_PER_IMAGE = SIDE // BANK_ROWS
-VECTOR_PIXELS = VECTOR_ROWS * SIDE
-TENSOR_PIXELS = TENSOR_ROWS * SIDE
-PAD_ROWS = SIDE + BANK_ROWS
+PAIRS = BANKS_PER_IMAGE - 1
+PAIR_PIXELS = PAIR * SIDE
 
 
 def tile_qca_operator_deep_pa_t_kernel(tc, x_cat, w1_words, w1_scales, out):
@@ -64,8 +62,7 @@ def tile_qca_operator_deep_pa_t_kernel(tc, x_cat, w1_words, w1_scales, out):
         psum_nbr = stack.enter_context(tc.psum_pool(name="psum_nbr", bufs=2))
         psum_acc = stack.enter_context(tc.psum_pool(name="psum_acc", bufs=4))
 
-        x_pad = keep.tile([P, IMAGES, PAD_ROWS, SIDE], BF16, name="x_pad")
-        nc.gpsimd.memset(x_pad[:, :, 0 : SIDE + 2 : SIDE + 1, :], 0.0)
+        x_pad = keep.tile([P, IMAGES, SIDE, SIDE], BF16, name="x_pad")
         w_codes = keep.tile([P, WORDS, HALVES, 2 * HID], U8, name="w_codes", align_bytes=64)
         w_planes = keep.tile([P, HALVES, HID], U8, name="w_planes", align_bytes=64)
         ident = keep.tile([P, P], BF16, name="ident")
@@ -76,14 +73,15 @@ def tile_qca_operator_deep_pa_t_kernel(tc, x_cat, w1_words, w1_scales, out):
         def load_rows(b, first, count):
             for d in range(HALVES):
                 nc.sync.dma_start(
-                    out=x_pad[d::HALVES, b, 1 + first : 1 + first + count, :].rearrange("c i j -> c (i j)"),
+                    out=x_pad[d::HALVES, b, first : first + count, :].rearrange("c i j -> c (i j)"),
                     in_=x_cat[b, :, first : first + count, :].rearrange(
                         "(g d m) i j -> d g m (i j)", g=GROUPS, d=HALVES
                     )[d],
                 )
 
-        for part in range(CHUNKS_PER_IMAGE):
-            load_rows(0, part * CHUNK_ROWS, CHUNK_ROWS)
+        load_rows(0, 0, CHUNK_ROWS + PAIR)
+        load_rows(0, CHUNK_ROWS + PAIR, SIDE // 2 - CHUNK_ROWS)
+        load_rows(0, SIDE // 2 + PAIR, SIDE // 2 - PAIR)
         for g in range(GROUPS):
             for d in range(HALVES):
                 nc.sync.dma_start(
@@ -102,9 +100,9 @@ def tile_qca_operator_deep_pa_t_kernel(tc, x_cat, w1_words, w1_scales, out):
             load_rows(b, 0, SIDE)
 
         col_sum = {}
-        for banks in (2, 6, 8):
-            col_sum[banks] = keep.tile([P, banks * VECTOR_ROWS * PITCH + 2], F32, name="col_sum%d" % banks)
-            nc.gpsimd.memset(col_sum[banks][:, 0 : banks * VECTOR_ROWS * PITCH + 1 : PITCH], 0.0)
+        for banks in (2, 5, 7):
+            col_sum[banks] = keep.tile([P, banks * PAIR * PITCH + 2], F32, name="col_sum%d" % banks)
+            nc.gpsimd.memset(col_sum[banks][:, 0 : banks * PAIR * PITCH + 1 : PITCH], 0.0)
         ident_pad = keep.tile([P, PATCH_ROWS, PATCH_COLS + 2], BF16, name="ident_pad")
         nc.vector.memset(ident_pad[:], 0.0)
         nc.vector.tensor_copy(
@@ -114,14 +112,17 @@ def tile_qca_operator_deep_pa_t_kernel(tc, x_cat, w1_words, w1_scales, out):
         nc.vector.tensor_tensor(
             out=beside[:], in0=ident_pad[:, :, 0:PATCH_COLS], in1=ident_pad[:, :, 2 : PATCH_COLS + 2], op=ADD
         )
-        around = keep.tile([P, PATCH_ROWS, PATCH_COLS], BF16, name="around")
-        nc.vector.tensor_tensor(out=around[:], in0=beside[:], in1=ident_pad[:, :, 1 : PATCH_COLS + 1], op=ADD)
-        outer = keep.tile([P, TENSOR_ROWS, PATCH_COLS], BF16, name="outer")
+        around = keep.tile([P, PATCH_ROWS + 2, PATCH_COLS], BF16, name="around")
+        nc.vector.memset(around[:], 0.0)
         nc.vector.tensor_tensor(
-            out=outer[:], in0=around[:, 0:TENSOR_ROWS, :], in1=around[:, 2 : TENSOR_ROWS + 2, :], op=ADD
+            out=around[:, 1 : PATCH_ROWS + 1, :], in0=beside[:], in1=ident_pad[:, :, 1 : PATCH_COLS + 1], op=ADD
         )
-        window = keep.tile([P, TENSOR_ROWS, PATCH_COLS], BF16, name="window")
-        nc.vector.tensor_tensor(out=window[:], in0=outer[:], in1=beside[:, 1 : TENSOR_ROWS + 1, :], op=ADD)
+        outer = keep.tile([P, PATCH_ROWS, PATCH_COLS], BF16, name="outer")
+        nc.vector.tensor_tensor(
+            out=outer[:], in0=around[:, 0:PATCH_ROWS, :], in1=around[:, 2 : PATCH_ROWS + 2, :], op=ADD
+        )
+        window = keep.tile([P, PATCH_ROWS, PATCH_COLS], BF16, name="window")
+        nc.vector.tensor_tensor(out=window[:], in0=outer[:], in1=beside[:], op=ADD)
 
         above_below = {}
         left_right = {}
@@ -134,23 +135,23 @@ def tile_qca_operator_deep_pa_t_kernel(tc, x_cat, w1_words, w1_scales, out):
         neg = {}
 
         def rows_of(flat):
-            return flat.rearrange("p (g r j) -> p g r j", r=VECTOR_ROWS, j=SIDE)
+            return flat.rearrange("p (g r j) -> p g r j", r=PAIR, j=SIDE)
 
         def column_sums(batch, shift):
             banks = batch[2]
-            return col_sum[banks][:, shift : shift + banks * VECTOR_ROWS * PITCH].rearrange(
-                "p (g r j) -> p g r j", r=VECTOR_ROWS, j=PITCH
+            return col_sum[banks][:, shift : shift + banks * PAIR * PITCH].rearrange(
+                "p (g r j) -> p g r j", r=PAIR, j=PITCH
             )[:, :, :, 0:SIDE]
 
         def padded_rows(batch, offset):
-            b, first, banks = batch
-            top = first * BANK_ROWS + TENSOR_ROWS + offset
-            return x_pad[:, b, top : top + banks * BANK_ROWS, :].rearrange("p (g r) j -> p g r j", r=BANK_ROWS)[
-                :, :, 0:VECTOR_ROWS, :
+            b, first, count = batch
+            top = first * BANK_ROWS - 2 + offset
+            return x_pad[:, b, top : top + count * BANK_ROWS, :].rearrange("p (g r) j -> p g r j", r=BANK_ROWS)[
+                :, :, 0:PAIR, :
             ]
 
         def add_above_and_below(batch):
-            above_below[batch] = sums.tile([P, batch[2] * VECTOR_PIXELS], F32, name="above_below")
+            above_below[batch] = sums.tile([P, batch[2] * PAIR_PIXELS], F32, name="above_below")
             nc.vector.tensor_tensor(
                 out=rows_of(above_below[batch][:]), in0=padded_rows(batch, 0), in1=padded_rows(batch, 2), op=ADD
             )
@@ -161,17 +162,21 @@ def tile_qca_operator_deep_pa_t_kernel(tc, x_cat, w1_words, w1_scales, out):
             )
 
         def add_left_and_right(batch):
-            left_right[batch] = sums.tile([P, batch[2] * VECTOR_PIXELS], F32, name="left_right")
+            left_right[batch] = sums.tile([P, batch[2] * PAIR_PIXELS], F32, name="left_right")
             nc.vector.tensor_tensor(
                 out=rows_of(left_right[batch][:]), in0=column_sums(batch, 0), in1=column_sums(batch, 2), op=ADD
             )
 
         def add_up_and_round(batch):
-            b, first, banks = batch
-            rounded = nbrs.tile([P, banks * VECTOR_PIXELS], BF16, name="rounded")
-            nc.vector.tensor_tensor(out=rounded[:], in0=left_right[batch][:], in1=above_below[batch][:], op=ADD)
-            for g in range(banks):
-                nbr[b, first + g] = rounded[:, g * VECTOR_PIXELS : (g + 1) * VECTOR_PIXELS]
+            b, first, count = batch
+            if b not in nbr:
+                nbr[b] = nbrs.tile([P, PAIRS * PAIR_PIXELS], BF16, name="rounded")
+            nc.vector.tensor_tensor(
+                out=nbr[b][:, (first - 1) * PAIR_PIXELS : (first - 1 + count) * PAIR_PIXELS],
+                in0=left_right[batch][:],
+                in1=above_below[batch][:],
+                op=ADD,
+            )
 
         add_steps = [add_above_and_below, add_centre, add_left_and_right, add_up_and_round]
 
@@ -195,6 +200,10 @@ def tile_qca_operator_deep_pa_t_kernel(tc, x_cat, w1_words, w1_scales, out):
 
         blocks_of = {}
 
+        def tensor_rows(n):
+            g = n % BANKS_PER_IMAGE
+            return (0 if g == 0 else 1, BANK_ROWS if g == BANKS_PER_IMAGE - 1 else BANK_ROWS - 1)
+
         def patches_on_scalar(n):
             return False
 
@@ -208,14 +217,15 @@ def tile_qca_operator_deep_pa_t_kernel(tc, x_cat, w1_words, w1_scales, out):
 
         def sum_on_tensor_engine(n):
             blocks = blocks_of[n]
-            nbr_acc[n] = psum_nbr.tile([P, TENSOR_ROWS, SIDE], F32, name="nbr_acc")
+            nbr_acc[n] = psum_nbr.tile([P, BANK_ROWS, SIDE], F32, name="nbr_acc")
+            top, end = tensor_rows(n)
             for s in range(STRIPS):
                 lo = 0 if s == 0 else 1
                 hi = PATCH_COLS if s == STRIPS - 1 else STRIP_STEP + 1
                 nc.tensor.matmul(
-                    out=nbr_acc[n][:, :, s * STRIP_STEP + lo : s * STRIP_STEP + hi],
+                    out=nbr_acc[n][:, top:end, s * STRIP_STEP + lo : s * STRIP_STEP + hi],
                     lhsT=blocks[:, s, :],
-                    rhs=window[:, :, lo:hi],
+                    rhs=window[:, top:end, lo:hi],
                     start=True,
                     stop=True,
                 )
@@ -224,22 +234,31 @@ def tile_qca_operator_deep_pa_t_kernel(tc, x_cat, w1_words, w1_scales, out):
         def xn_tiles(n):
             xn[n] = moving.tile([P, BANK * PACK], BF16, name="xn", align_bytes=64)
 
+        def words_of_rows(n):
+            return xn[n][:].rearrange("p (i j t) -> p i j t", j=SIDE, t=PACK)
+
         def repeat_tensor_rows(n):
+            top, end = tensor_rows(n)
             nc.scalar.copy(
-                out=xn[n][:, 0 : TENSOR_PIXELS * PACK].rearrange("p (w t) -> p w t", t=PACK),
-                in_=nbr_acc[n][:]
-                .rearrange("p o j -> p (o j)")
-                .unsqueeze(2)
-                .to_broadcast([P, TENSOR_PIXELS, PACK]),
+                out=words_of_rows(n)[:, top:end],
+                in_=nbr_acc[n][:, top:end, :].unsqueeze(3).to_broadcast([P, end - top, SIDE, PACK]),
             )
 
         def repeat_vector_rows(n):
             copy = nc.vector.tensor_copy if repeats_on_vector(n) else nc.scalar.copy
+            b, g = divmod(n, BANKS_PER_IMAGE)
+            if g == 0:
+                rows, first, count = slice(BANK_ROWS - 1, BANK_ROWS), 0, 1
+            elif g == BANKS_PER_IMAGE - 1:
+                rows, first, count = slice(0, 1), 2 * PAIRS - 1, 1
+            else:
+                rows, first, count = slice(0, BANK_ROWS, BANK_ROWS - 1), 2 * g - 1, 2
             copy(
-                out=xn[n][:, TENSOR_PIXELS * PACK : BANK * PACK].rearrange("p (w t) -> p w t", t=PACK),
-                in_=nbr[divmod(n, BANKS_PER_IMAGE)]
-                .unsqueeze(2)
-                .to_broadcast([P, VECTOR_PIXELS, PACK]),
+                out=words_of_rows(n)[:, rows],
+                in_=nbr[b][:, first * SIDE : (first + count) * SIDE]
+                .rearrange("p (i j) -> p i j", j=SIDE)
+                .unsqueeze(3)
+                .to_broadcast([P, count, SIDE, PACK]),
             )
 
         codes = {}
@@ -267,28 +286,33 @@ def tile_qca_operator_deep_pa_t_kernel(tc, x_cat, w1_words, w1_scales, out):
                     stop=(w == WORDS - 1 and d == HALVES - 1),
                 )
 
-        one = {}
 
         def exponential(k, h):
             if h == 0:
-                neg[k] = tails.tile([HID, CHUNK], F32, name="neg")
-            nc.scalar.activation(out=neg[k][:, h * BANK : (h + 1) * BANK], in_=acc[2 * k + h][:], func=EXP)
+                neg[k] = tails.tile([HID, 1 + CHUNK], F32, name="neg")
+            nc.scalar.activation(out=neg[k][:, 1 + h * BANK : 1 + (h + 1) * BANK], in_=acc[2 * k + h][:], func=EXP)
 
         def on_gpsimd(k):
             return k < N_CHUNKS - 2
 
         def release_gpsimd(k):
-            one[k] = tails.tile([P, 1], F32, name="one")
-            nc.vector.memset(one[k][:], 1.0)
+            nc.vector.memset(neg[k][:, 0:1], 0.0)
 
-        def negative_part(k, h, scalar1=1.0, engine=nc.vector):
-            part = neg[k][:, h * BANK : (h + 1) * BANK]
-            engine.tensor_scalar(out=part, in0=part, scalar1=scalar1, scalar2=-1.0, op0=MIN, op1=ADD)
+        def minus_one(k, h, engine):
+            part = neg[k][:, 1 + h * BANK - (1 if h == 0 and engine is nc.gpsimd else 0) : 1 + (h + 1) * BANK]
+            engine.tensor_scalar(out=part, in0=part, scalar1=1.0, scalar2=-1.0, op0=MULT, op1=ADD)
 
         def finish(k, h):
             n = 2 * k + h
             res = results.tile([HID, BANK], F32, name="res")
-            nc.vector.tensor_tensor(out=res[:], in0=acc[n][:], in1=neg[k][:, h * BANK : (h + 1) * BANK], op=MAX)
+            nc.vector.scalar_tensor_tensor(
+                out=res[:],
+                in0=acc[n][:],
+                scalar=0.0,
+                in1=neg[k][:, 1 + h * BANK : 1 + (h + 1) * BANK],
+                op0=MAX,
+                op1=MIN,
+            )
             b, g = divmod(n, BANKS_PER_IMAGE)
             nc.sync.dma_start(
                 out=out[b, :, g * BANK_ROWS : (g + 1) * BANK_ROWS, :].rearrange("o i j -> o (i j)"), in_=res[:]
@@ -300,8 +324,8 @@ def tile_qca_operator_deep_pa_t_kernel(tc, x_cat, w1_words, w1_scales, out):
 
         LAG = 2
         with tc.manual_schedule():
-            first_chunk = (0, 0, BANKS_PER_CHUNK)
-            rest = (0, BANKS_PER_CHUNK, BANKS_PER_IMAGE - BANKS_PER_CHUNK)
+            first_chunk = (0, 1, 2)
+            rest = (0, 3, 5)
             for s in range(STRIPS):
                 copy_strip(0, s, 0, CHUNK_ROWS)
                 if s < 4:
@@ -347,10 +371,10 @@ def tile_qca_operator_deep_pa_t_kernel(tc, x_cat, w1_words, w1_scales, out):
                     multiply(2 * q + 1, 0)
                 if g_neg:
                     release_gpsimd(f)
-                    negative_part(f, 0, one[f][:], nc.gpsimd)
-                    negative_part(f, 1, one[f][:], nc.gpsimd)
+                    minus_one(f, 0, nc.gpsimd)
+                    minus_one(f, 1, nc.gpsimd)
                 if finishing and not g_neg:
-                    negative_part(f, 0)
+                    minus_one(f, 0, nc.vector)
                 if quantising:
                     quantise(2 * q + 1, 1)
                     multiply(2 * q + 1, 1)
@@ -362,7 +386,7 @@ def tile_qca_operator_deep_pa_t_kernel(tc, x_cat, w1_words, w1_scales, out):
                 if ahead:
                     copy_patches(2 * c + 3)
                 if finishing and not g_neg:
-                    negative_part(f, 1)
+                    minus_one(f, 1, nc.vector)
                 if c + 2 < N_CHUNKS:
                     transpose_patches(2 * c + 4)
                     transpose_patches(2 * c + 5)
@@ -381,7 +405,7 @@ def tile_qca_operator_deep_pa_t_kernel(tc, x_cat, w1_words, w1_scales, out):
                     add_steps[3](rest)
                 b, part = divmod(c, CHUNKS_PER_IMAGE)
                 if b + 1 < IMAGES:
-                    add_steps[part]((b + 1, 0, BANKS_PER_IMAGE))
+                    add_steps[part]((b + 1, 1, PAIRS))
                     if part < 2:
                         for s in range(3 * part, min(3 * part + 3, STRIPS)):
                             copy_strip(b + 1, s, 0, SIDE)

@@ -100,7 +100,7 @@ def tile_qca_operator_deep_pa_t_kernel(tc, x_cat, w1_words, w1_scales, out):
             load_rows(b, 0, SIDE)
 
         col_sum = {}
-        for banks in (2, 5, 7):
+        for banks in (2, 3, 4):
             col_sum[banks] = keep.tile([P, banks * PAIR * PITCH + 2], F32, name="col_sum%d" % banks)
             nc.gpsimd.memset(col_sum[banks][:, 0 : banks * PAIR * PITCH + 1 : PITCH], 0.0)
         ident_pad = keep.tile([P, PATCH_ROWS, PATCH_COLS + 2], BF16, name="ident_pad")
@@ -289,30 +289,17 @@ def tile_qca_operator_deep_pa_t_kernel(tc, x_cat, w1_words, w1_scales, out):
 
         def exponential(k, h):
             if h == 0:
-                neg[k] = tails.tile([HID, 1 + CHUNK], F32, name="neg")
-            nc.scalar.activation(out=neg[k][:, 1 + h * BANK : 1 + (h + 1) * BANK], in_=acc[2 * k + h][:], func=EXP)
+                neg[k] = tails.tile([HID, CHUNK], F32, name="neg")
+            nc.scalar.activation(out=neg[k][:, h * BANK : (h + 1) * BANK], in_=acc[2 * k + h][:], func=EXP)
 
-        def on_gpsimd(k):
-            return k < N_CHUNKS - 2
-
-        def release_gpsimd(k):
-            nc.vector.memset(neg[k][:, 0:1], 0.0)
-
-        def minus_one(k, h, engine):
-            part = neg[k][:, 1 + h * BANK - (1 if h == 0 and engine is nc.gpsimd else 0) : 1 + (h + 1) * BANK]
-            engine.tensor_scalar(out=part, in0=part, scalar1=1.0, scalar2=-1.0, op0=MULT, op1=ADD)
+        def minus_one(k, lo=0, hi=BANKS_PER_CHUNK):
+            part = neg[k][:, lo * BANK : hi * BANK]
+            nc.vector.tensor_scalar(out=part, in0=part, scalar1=1.0, scalar2=-1.0, op0=MIN, op1=ADD)
 
         def finish(k, h):
             n = 2 * k + h
             res = results.tile([HID, BANK], F32, name="res")
-            nc.vector.scalar_tensor_tensor(
-                out=res[:],
-                in0=acc[n][:],
-                scalar=0.0,
-                in1=neg[k][:, 1 + h * BANK : 1 + (h + 1) * BANK],
-                op0=MAX,
-                op1=MIN,
-            )
+            nc.vector.tensor_tensor(out=res[:], in0=acc[n][:], in1=neg[k][:, h * BANK : (h + 1) * BANK], op=MAX)
             b, g = divmod(n, BANKS_PER_IMAGE)
             nc.sync.dma_start(
                 out=out[b, :, g * BANK_ROWS : (g + 1) * BANK_ROWS, :].rearrange("o i j -> o (i j)"), in_=res[:]
@@ -325,7 +312,8 @@ def tile_qca_operator_deep_pa_t_kernel(tc, x_cat, w1_words, w1_scales, out):
         LAG = 2
         with tc.manual_schedule():
             first_chunk = (0, 1, 2)
-            rest = (0, 3, 5)
+            second_chunk = (0, 3, 2)
+            halves = [(1, 4), (5, 3)]
             for s in range(STRIPS):
                 copy_strip(0, s, 0, CHUNK_ROWS)
                 if s < 4:
@@ -343,7 +331,7 @@ def tile_qca_operator_deep_pa_t_kernel(tc, x_cat, w1_words, w1_scales, out):
                 copy_strip(0, s, CHUNK_ROWS, SIDE - CHUNK_ROWS)
             transpose_patches(2)
             transpose_patches(3)
-            add_steps[0](rest)
+            add_steps[0](second_chunk)
             for c in range(N_CHUNKS + LAG + 1):
                 q = c - LAG
                 f = q - 1
@@ -354,39 +342,47 @@ def tile_qca_operator_deep_pa_t_kernel(tc, x_cat, w1_words, w1_scales, out):
                 if finishing:
                     exponential(f, 0)
                     exponential(f, 1)
-                if summing:
-                    for h in range(2):
+                for h in range(2):
+                    if ahead and patches_on_scalar(2 * c + 2 + h):
+                        copy_patches(2 * c + 2 + h)
+                    if summing:
                         n = 2 * c + h
                         xn_tile(n)
                         repeat_tensor_rows(n)
                         if c > 0 and not repeats_on_vector(n):
                             repeat_vector_rows(n)
-                g_neg = finishing and on_gpsimd(f)
+                half, stage = divmod(c + 2, 2)
+                b, second = divmod(half, 2)
+                due = None
+                if 0 < half and b < IMAGES:
+                    due = ((b,) + halves[second], 2 * stage)
                 if quantising:
                     quantise(2 * q, 0)
                     multiply(2 * q, 0)
                     quantise(2 * q, 1)
                     multiply(2 * q, 1)
+                if due:
+                    add_steps[due[1]](due[0])
+                if quantising:
                     quantise(2 * q + 1, 0)
                     multiply(2 * q + 1, 0)
-                if g_neg:
-                    release_gpsimd(f)
-                    minus_one(f, 0, nc.gpsimd)
-                    minus_one(f, 1, nc.gpsimd)
-                if finishing and not g_neg:
-                    minus_one(f, 0, nc.vector)
+                if finishing and f < N_CHUNKS - 1:
+                    minus_one(f)
+                elif finishing:
+                    minus_one(f, 0, 1)
                 if quantising:
                     quantise(2 * q + 1, 1)
                     multiply(2 * q + 1, 1)
                 if ahead:
-                    copy_patches(2 * c + 2)
+                    if not patches_on_scalar(2 * c + 2):
+                        copy_patches(2 * c + 2)
                     sum_on_tensor_engine(2 * c + 2)
                 if c == 0:
-                    add_steps[1](rest)
-                if ahead:
+                    add_steps[1](second_chunk)
+                if ahead and not patches_on_scalar(2 * c + 3):
                     copy_patches(2 * c + 3)
-                if finishing and not g_neg:
-                    minus_one(f, 1, nc.vector)
+                if f == N_CHUNKS - 1:
+                    minus_one(f, 1, 2)
                 if c + 2 < N_CHUNKS:
                     transpose_patches(2 * c + 4)
                     transpose_patches(2 * c + 5)
@@ -401,11 +397,13 @@ def tile_qca_operator_deep_pa_t_kernel(tc, x_cat, w1_words, w1_scales, out):
                     finish(f, 0)
                     finish(f, 1)
                 if c == 0:
-                    add_steps[2](rest)
-                    add_steps[3](rest)
+                    add_steps[2](second_chunk)
+                    add_steps[3](second_chunk)
+                if due:
+                    add_steps[due[1] + 1](due[0])
                 b, part = divmod(c, CHUNKS_PER_IMAGE)
                 if b + 1 < IMAGES:
-                    add_steps[part]((b + 1, 1, PAIRS))
-                    if part < 2:
-                        for s in range(3 * part, min(3 * part + 3, STRIPS)):
+                    strips_first = [0,2,5]
+                    if part + 1 < len(strips_first):
+                        for s in range(strips_first[part], strips_first[part + 1]):
                             copy_strip(b + 1, s, 0, SIDE)

@@ -71,13 +71,15 @@ def tile_qca_operator_deep_pa_t_kernel(tc, x_cat, w1_words, w1_scales, out):
         nc.gpsimd.memset(w_planes[:].rearrange("p d n -> p (d n)").bitcast(I32), 0)
 
         def load_rows(b, first, count):
-            for d in range(HALVES):
-                nc.sync.dma_start(
-                    out=x_pad[d::HALVES, b, first : first + count, :].rearrange("c i j -> c (i j)"),
-                    in_=x_cat[b, :, first : first + count, :].rearrange(
-                        "(g d m) i j -> d g m (i j)", g=GROUPS, d=HALVES
-                    )[d],
-                )
+            for g in range(GROUPS):
+                for d in range(HALVES):
+                    channel = 64 * g + 32 * d
+                    nc.sync.dma_start(
+                        out=x_pad[64 * g + d : 64 * (g + 1) : 2, b, first : first + count, :].rearrange(
+                            "c i j -> c (i j)"
+                        ),
+                        in_=x_cat[b, channel : channel + 32, first : first + count, :].rearrange("c i j -> c (i j)"),
+                    )
 
         load_rows(0, 0, CHUNK_ROWS + PAIR)
         load_rows(0, CHUNK_ROWS + PAIR, SIDE // 2 - CHUNK_ROWS)

@@ -207,10 +207,13 @@ def tile_qca_operator_deep_pa_t_kernel(tc, x_cat, w1_words, w1_scales, out):
             return (0 if g == 0 else 1, BANK_ROWS if g == BANKS_PER_IMAGE - 1 else BANK_ROWS - 1)
 
         def patches_on_scalar(n):
+            return n > 3
+
+        def tensor_rows_on_vector(n):
             return False
 
         def repeats_on_vector(n):
-            return False
+            return n % 2 == 1
 
         def copy_patches(n):
             blocks_of[n] = patches.tile([P, STRIPS, P], BF16, name="blocks")
@@ -241,7 +244,8 @@ def tile_qca_operator_deep_pa_t_kernel(tc, x_cat, w1_words, w1_scales, out):
 
         def repeat_tensor_rows(n):
             top, end = tensor_rows(n)
-            nc.scalar.copy(
+            copy = nc.vector.tensor_copy if tensor_rows_on_vector(n) else nc.scalar.copy
+            copy(
                 out=words_of_rows(n)[:, top:end],
                 in_=nbr_acc[n][:, top:end, :].unsqueeze(3).to_broadcast([P, end - top, SIDE, PACK]),
             )
@@ -298,10 +302,24 @@ def tile_qca_operator_deep_pa_t_kernel(tc, x_cat, w1_words, w1_scales, out):
             part = neg[k][:, lo * BANK : hi * BANK]
             nc.vector.tensor_scalar(out=part, in0=part, scalar1=1.0, scalar2=-1.0, op0=MIN, op1=ADD)
 
+        def scalar_takes(k):
+            return k >= N_CHUNKS - 2
+
+        def one_minus(k, h):
+            part = neg[k][:, h * BANK : (h + 1) * BANK]
+            nc.scalar.activation(out=part, in_=part, func=RELU, bias=1.0, scale=-1.0)
+
         def finish(k, h):
             n = 2 * k + h
             res = results.tile([HID, BANK], F32, name="res")
-            nc.vector.tensor_tensor(out=res[:], in0=acc[n][:], in1=neg[k][:, h * BANK : (h + 1) * BANK], op=MAX)
+            nc.vector.scalar_tensor_tensor(
+                out=res[:],
+                in0=neg[k][:, h * BANK : (h + 1) * BANK],
+                scalar=-1.0 if scalar_takes(k) else 1.0,
+                in1=acc[n][:],
+                op0=MULT,
+                op1=MAX,
+            )
             b, g = divmod(n, BANKS_PER_IMAGE)
             nc.sync.dma_start(
                 out=out[b, :, g * BANK_ROWS : (g + 1) * BANK_ROWS, :].rearrange("o i j -> o (i j)"), in_=res[:]
@@ -311,101 +329,105 @@ def tile_qca_operator_deep_pa_t_kernel(tc, x_cat, w1_words, w1_scales, out):
             if n not in xn:
                 xn[n] = moving.tile([P, BANK * PACK], BF16, name="xn", align_bytes=64)
 
-        LAG = 2
         with tc.manual_schedule():
             first_chunk = (0, 1, 2)
             second_chunk = (0, 3, 2)
             halves = [(1, 4), (5, 3)]
             for s in range(STRIPS):
                 copy_strip(0, s, 0, CHUNK_ROWS)
-                if s < 4:
-                    add_steps[s](first_chunk)
             transpose_patches(0)
             transpose_patches(1)
-            for n in range(2):
-                xn_tile(n)
-                repeat_vector_rows(n)
+            add_steps[0](first_chunk)
             copy_patches(0)
             sum_on_tensor_engine(0)
+            add_steps[1](first_chunk)
             copy_patches(1)
             sum_on_tensor_engine(1)
+            add_steps[2](first_chunk)
             for s in range(STRIPS):
                 copy_strip(0, s, CHUNK_ROWS, SIDE - CHUNK_ROWS)
+                if s == 1:
+                    add_steps[3](first_chunk)
             transpose_patches(2)
             transpose_patches(3)
             add_steps[0](second_chunk)
-            for c in range(N_CHUNKS + LAG + 1):
-                q = c - LAG
-                f = q - 1
+            for c in range(N_CHUNKS + 2):
+                q = c - 1
+                f = c - 2
                 summing = c < N_CHUNKS
                 ahead = c + 1 < N_CHUNKS
                 quantising = 0 <= q < N_CHUNKS
                 finishing = 0 <= f
-                if finishing:
-                    exponential(f, 0)
-                    exponential(f, 1)
-                for h in range(2):
-                    if ahead and patches_on_scalar(2 * c + 2 + h):
-                        copy_patches(2 * c + 2 + h)
-                    if summing:
-                        n = 2 * c + h
-                        xn_tile(n)
-                        repeat_tensor_rows(n)
-                        if c > 0 and not repeats_on_vector(n):
-                            repeat_vector_rows(n)
                 half, stage = divmod(c + 2, 2)
                 b, second = divmod(half, 2)
-                due = None
-                if 0 < half and b < IMAGES:
-                    due = ((b,) + halves[second], 2 * stage)
-                if quantising:
-                    quantise(2 * q, 0)
-                    multiply(2 * q, 0)
-                    quantise(2 * q, 1)
-                    multiply(2 * q, 1)
-                if due:
-                    add_steps[due[1]](due[0])
-                if quantising:
-                    quantise(2 * q + 1, 0)
-                    multiply(2 * q + 1, 0)
-                if finishing and f < N_CHUNKS - 1:
-                    minus_one(f)
-                elif finishing:
-                    minus_one(f, 0, 1)
-                if quantising:
-                    quantise(2 * q + 1, 1)
-                    multiply(2 * q + 1, 1)
-                if ahead:
-                    if not patches_on_scalar(2 * c + 2):
-                        copy_patches(2 * c + 2)
-                    sum_on_tensor_engine(2 * c + 2)
+                due = []
+                if b < IMAGES:
+                    due = [(2 * stage + i, (b,) + halves[second]) for i in range(2)]
+                for h in range(2):
+                    n = 2 * c + h
+                    if finishing:
+                        exponential(f, h)
+                        if scalar_takes(f):
+                            one_minus(f, h)
+                    if ahead and patches_on_scalar(n + 2):
+                        copy_patches(n + 2)
+                    if summing:
+                        xn_tile(n)
+                        if not tensor_rows_on_vector(n):
+                            repeat_tensor_rows(n)
+                        if c > 0 and not repeats_on_vector(n):
+                            repeat_vector_rows(n)
+                if c == 0:
+                    repeat_vector_rows(0)
+                    repeat_vector_rows(1)
+
+                def look_ahead():
+                    if ahead:
+                        sum_on_tensor_engine(2 * c + 2)
+                    if c + 2 < N_CHUNKS:
+                        transpose_patches(2 * c + 4)
+                        transpose_patches(2 * c + 5)
+                    if ahead:
+                        sum_on_tensor_engine(2 * c + 3)
+
                 if c == 0:
                     add_steps[1](second_chunk)
-                if ahead and not patches_on_scalar(2 * c + 3):
-                    copy_patches(2 * c + 3)
-                if f == N_CHUNKS - 1:
-                    minus_one(f, 1, 2)
-                if c + 2 < N_CHUNKS:
-                    transpose_patches(2 * c + 4)
-                    transpose_patches(2 * c + 5)
-                if ahead:
-                    sum_on_tensor_engine(2 * c + 3)
+                for step, batch in due[0:1]:
+                    add_steps[step](batch)
+                if quantising:
+                    for w in range(2):
+                        quantise(2 * q, w)
+                        multiply(2 * q, w)
+                for h in range(2):
+                    if ahead and not patches_on_scalar(2 * c + 2 + h):
+                        copy_patches(2 * c + 2 + h)
+                    if c == 0:
+                        add_steps[2 + h](second_chunk)
+                look_ahead()
+                part = c % CHUNKS_PER_IMAGE
+                b = c // CHUNKS_PER_IMAGE + 1
+                if b < IMAGES:
+                    for s in range(STRIPS):
+                        if part == (0 if s < 2 else 1):
+                            copy_strip(b, s, 0, SIDE)
+                if quantising:
+                    for w in range(2):
+                        quantise(2 * q + 1, w)
+                        multiply(2 * q + 1, w)
+
+                if finishing and f < N_CHUNKS - 1 and not scalar_takes(f):
+                    minus_one(f)
+                for step, batch in due[-1:]:
+                    add_steps[step](batch)
                 if summing:
                     for h in range(2):
                         n = 2 * c + h
+                        if tensor_rows_on_vector(n):
+                            repeat_tensor_rows(n)
                         if c > 0 and repeats_on_vector(n):
                             repeat_vector_rows(n)
                 if finishing:
-                    finish(f, 0)
-                    finish(f, 1)
-                if c == 0:
-                    add_steps[2](second_chunk)
-                    add_steps[3](second_chunk)
-                if due:
-                    add_steps[due[1] + 1](due[0])
-                b, part = divmod(c, CHUNKS_PER_IMAGE)
-                if b + 1 < IMAGES:
-                    strips_first = [0,2,5]
-                    if part + 1 < len(strips_first):
-                        for s in range(strips_first[part], strips_first[part + 1]):
-                            copy_strip(b + 1, s, 0, SIDE)
+                    for h in range(2):
+                        if f == N_CHUNKS - 1 and not scalar_takes(f):
+                            minus_one(f, h, h + 1)
+                        finish(f, h)

@@ -192,10 +192,10 @@ def tile_qca_operator_deep_pa_t_kernel(tc, x_cat, w1_words, w1_scales, out):
 
         def transpose_patches(n):
             b, g = divmod(n, BANKS_PER_IMAGE)
-            flipped[n] = psum_flip.tile([P, STRIPS, P], BF16, name="flipped")
+            flipped[n] = psum_flip.tile([P, STRIPS * P], BF16, name="flipped")
             for s in range(STRIPS):
                 nc.tensor.transpose(
-                    flipped[n][:, s, :],
+                    flipped[n][:, s * P : (s + 1) * P],
                     strips[b][:, s, g * BANK_ROWS : g * BANK_ROWS + PATCH_ROWS, :].rearrange("p i j -> p (i j)"),
                     ident[:],
                 )
@@ -216,7 +216,7 @@ def tile_qca_operator_deep_pa_t_kernel(tc, x_cat, w1_words, w1_scales, out):
             return n % 2 == 1
 
         def copy_patches(n):
-            blocks_of[n] = patches.tile([P, STRIPS, P], BF16, name="blocks")
+            blocks_of[n] = patches.tile([P, STRIPS * P], BF16, name="blocks")
             copy = nc.scalar.copy if patches_on_scalar(n) else nc.vector.tensor_copy
             copy(out=blocks_of[n][:], in_=flipped[n][:])
 
@@ -229,7 +229,7 @@ def tile_qca_operator_deep_pa_t_kernel(tc, x_cat, w1_words, w1_scales, out):
                 hi = PATCH_COLS if s == STRIPS - 1 else STRIP_STEP + 1
                 nc.tensor.matmul(
                     out=nbr_acc[n][:, top:end, s * STRIP_STEP + lo : s * STRIP_STEP + hi],
-                    lhsT=blocks[:, s, :],
+                    lhsT=blocks[:, s * P : (s + 1) * P],
                     rhs=window[:, top:end, lo:hi],
                     start=True,
                     stop=True,
@@ -381,51 +381,59 @@ def tile_qca_operator_deep_pa_t_kernel(tc, x_cat, w1_words, w1_scales, out):
                     repeat_vector_rows(0)
                     repeat_vector_rows(1)
 
-                def look_ahead():
-                    if ahead:
-                        sum_on_tensor_engine(2 * c + 2)
-                    if c + 2 < N_CHUNKS:
-                        transpose_patches(2 * c + 4)
-                        transpose_patches(2 * c + 5)
-                    if ahead:
-                        sum_on_tensor_engine(2 * c + 3)
+                part = c % CHUNKS_PER_IMAGE
+                image = c // CHUNKS_PER_IMAGE + 1
 
+                def own_rows(h):
+                    n = 2 * c + h
+                    if summing and tensor_rows_on_vector(n):
+                        repeat_tensor_rows(n)
+                    if summing and c > 0 and repeats_on_vector(n):
+                        repeat_vector_rows(n)
+
+                def strips_due(lo, hi):
+                    if image < IMAGES:
+                        for s in range(STRIPS):
+                            if part == (0 if s < 2 else 1) and lo <= s < hi:
+                                copy_strip(image, s, 0, SIDE)
+
+                if quantising:
+                    quantise(2 * q, 0)
+                    multiply(2 * q, 0)
                 if c == 0:
                     add_steps[1](second_chunk)
                 for step, batch in due[0:1]:
                     add_steps[step](batch)
+                own_rows(0)
                 if quantising:
-                    for w in range(2):
-                        quantise(2 * q, w)
-                        multiply(2 * q, w)
+                    quantise(2 * q, 1)
+                    multiply(2 * q, 1)
                 for h in range(2):
                     if ahead and not patches_on_scalar(2 * c + 2 + h):
                         copy_patches(2 * c + 2 + h)
                     if c == 0:
                         add_steps[2 + h](second_chunk)
-                look_ahead()
-                part = c % CHUNKS_PER_IMAGE
-                b = c // CHUNKS_PER_IMAGE + 1
-                if b < IMAGES:
-                    for s in range(STRIPS):
-                        if part == (0 if s < 2 else 1):
-                            copy_strip(b, s, 0, SIDE)
+                if ahead:
+                    sum_on_tensor_engine(2 * c + 2)
+                if c + 2 < N_CHUNKS:
+                    transpose_patches(2 * c + 4)
+                strips_due(0, 3)
+                for step, batch in due[1:2]:
+                    add_steps[step](batch)
                 if quantising:
-                    for w in range(2):
-                        quantise(2 * q + 1, w)
-                        multiply(2 * q + 1, w)
-
+                    quantise(2 * q + 1, 0)
+                    multiply(2 * q + 1, 0)
                 if finishing and f < N_CHUNKS - 1 and not scalar_takes(f):
                     minus_one(f)
-                for step, batch in due[-1:]:
-                    add_steps[step](batch)
-                if summing:
-                    for h in range(2):
-                        n = 2 * c + h
-                        if tensor_rows_on_vector(n):
-                            repeat_tensor_rows(n)
-                        if c > 0 and repeats_on_vector(n):
-                            repeat_vector_rows(n)
+                own_rows(1)
+                if quantising:
+                    quantise(2 * q + 1, 1)
+                    multiply(2 * q + 1, 1)
+                strips_due(3, STRIPS)
+                if c + 2 < N_CHUNKS:
+                    transpose_patches(2 * c + 5)
+                if ahead:
+                    sum_on_tensor_engine(2 * c + 3)
                 if finishing:
                     for h in range(2):
                         if f == N_CHUNKS - 1 and not scalar_takes(f):

@@ -72,33 +72,30 @@ def tile_qca_operator_deep_pa_t_kernel(tc, x_cat, w1_words, w1_scales, out):
 
         def load_rows(b, first, count):
             for g in range(GROUPS):
-                for d in range(HALVES):
-                    channel = 64 * g + 32 * d
-                    nc.sync.dma_start(
-                        out=x_pad[64 * g + d : 64 * (g + 1) : 2, b, first : first + count, :].rearrange(
-                            "c i j -> c (i j)"
-                        ),
-                        in_=x_cat[b, channel : channel + 32, first : first + count, :].rearrange("c i j -> c (i j)"),
-                    )
+                nc.sync.dma_start(
+                    out=x_pad[64 * g : 64 * (g + 1), b, first : first + count, :].rearrange("c i j -> c (i j)"),
+                    in_=x_cat[b, 64 * g : 64 * (g + 1), first : first + count, :].rearrange(
+                        "(d m) i j -> m d (i j)", d=HALVES
+                    ),
+                )
 
         load_rows(0, 0, CHUNK_ROWS + PAIR)
         load_rows(0, CHUNK_ROWS + PAIR, SIDE // 2 - CHUNK_ROWS)
         load_rows(0, SIDE // 2 + PAIR, SIDE // 2 - PAIR)
+        load_rows(1, 0, SIDE)
         for g in range(GROUPS):
             for d in range(HALVES):
                 nc.sync.dma_start(
                     out=w_codes[64 * g + d : 64 * (g + 1) : 2, :, d, :].bitcast(I32),
                     in_=w1_words[g, 64 * d : 64 * (d + 1), :].rearrange("(m h) n -> m h n", h=WORDS).bitcast(I32),
                 )
-        for d in range(HALVES):
-            for quadrant in range(4):
-                g, first = divmod(quadrant, 2)
-                row = 8 * d + 4 * first
-                nc.sync.dma_start(
-                    out=w_planes[32 * quadrant : 32 * quadrant + 4, d, :].bitcast(I32),
-                    in_=w1_scales[g, row : row + 4, :].bitcast(I32),
-                )
-        for b in range(1, IMAGES):
+        for quadrant in range(4):
+            g, f = divmod(quadrant, 2)
+            nc.sync.dma_start(
+                out=w_planes[32 * quadrant : 32 * quadrant + 4, :, :].bitcast(I32),
+                in_=w1_scales[g].rearrange("(d f e) n -> f e d n", d=HALVES, f=2)[f].bitcast(I32),
+            )
+        for b in range(2, IMAGES):
             load_rows(b, 0, SIDE)
 
         col_sum = {}
@@ -182,10 +179,10 @@ def tile_qca_operator_deep_pa_t_kernel(tc, x_cat, w1_words, w1_scales, out):
 
         add_steps = [add_above_and_below, add_centre, add_left_and_right, add_up_and_round]
 
-        def copy_strip(b, s, first, count):
+        def copy_strip(b, s, first, count, copy=nc.vector.tensor_copy):
             if b not in strips:
                 strips[b] = strip_pool.tile([P, STRIPS, SIDE, PATCH_COLS], BF16, name="strips")
-            nc.vector.tensor_copy(
+            copy(
                 out=strips[b][:, s, first : first + count, :],
                 in_=x_pad[:, b, first : first + count, s * STRIP_STEP : s * STRIP_STEP + PATCH_COLS],
             )
@@ -213,7 +210,7 @@ def tile_qca_operator_deep_pa_t_kernel(tc, x_cat, w1_words, w1_scales, out):
             return False
 
         def repeats_on_vector(n):
-            return n % 2 == 1
+            return n % 2 == 1 or n >= 28
 
         def copy_patches(n):
             blocks_of[n] = patches.tile([P, STRIPS * P], BF16, name="blocks")
@@ -293,36 +290,38 @@ def tile_qca_operator_deep_pa_t_kernel(tc, x_cat, w1_words, w1_scales, out):
                 )
 
 
-        def exponential(k, h):
+        def exponential(k, h, lo=0, hi=BANK):
             if h == 0:
                 neg[k] = tails.tile([HID, CHUNK], F32, name="neg")
-            nc.scalar.activation(out=neg[k][:, h * BANK : (h + 1) * BANK], in_=acc[2 * k + h][:], func=EXP)
+            nc.scalar.activation(
+                out=neg[k][:, h * BANK + lo : h * BANK + hi], in_=acc[2 * k + h][:, lo:hi], func=EXP
+            )
 
-        def minus_one(k, lo=0, hi=BANKS_PER_CHUNK):
-            part = neg[k][:, lo * BANK : hi * BANK]
+        def minus_one(k, lo=0, hi=CHUNK):
+            part = neg[k][:, lo:hi]
             nc.vector.tensor_scalar(out=part, in0=part, scalar1=1.0, scalar2=-1.0, op0=MIN, op1=ADD)
 
         def scalar_takes(k):
-            return k >= N_CHUNKS - 2
+            return k == N_CHUNKS - 2
 
         def one_minus(k, h):
             part = neg[k][:, h * BANK : (h + 1) * BANK]
             nc.scalar.activation(out=part, in_=part, func=RELU, bias=1.0, scale=-1.0)
 
-        def finish(k, h):
+        def finish(k, h, lo=0, hi=BANK):
             n = 2 * k + h
-            res = results.tile([HID, BANK], F32, name="res")
+            res = results.tile([HID, hi - lo], F32, name="res")
             nc.vector.scalar_tensor_tensor(
                 out=res[:],
-                in0=neg[k][:, h * BANK : (h + 1) * BANK],
+                in0=neg[k][:, h * BANK + lo : h * BANK + hi],
                 scalar=-1.0 if scalar_takes(k) else 1.0,
-                in1=acc[n][:],
+                in1=acc[n][:, lo:hi],
                 op0=MULT,
                 op1=MAX,
             )
             b, g = divmod(n, BANKS_PER_IMAGE)
             nc.sync.dma_start(
-                out=out[b, :, g * BANK_ROWS : (g + 1) * BANK_ROWS, :].rearrange("o i j -> o (i j)"), in_=res[:]
+                out=out[b, :, g * BANK_ROWS : (g + 1) * BANK_ROWS, :].rearrange("o i j -> o (i j)")[:, lo:hi], in_=res[:]
             )
 
         def xn_tile(n):
@@ -345,13 +344,13 @@ def tile_qca_operator_deep_pa_t_kernel(tc, x_cat, w1_words, w1_scales, out):
             sum_on_tensor_engine(1)
             add_steps[2](first_chunk)
             for s in range(STRIPS):
-                copy_strip(0, s, CHUNK_ROWS, SIDE - CHUNK_ROWS)
-                if s == 1:
+                copy_strip(0, s, CHUNK_ROWS, SIDE - CHUNK_ROWS, nc.scalar.copy if s < 2 else nc.vector.tensor_copy)
+                if s == 3:
                     add_steps[3](first_chunk)
             transpose_patches(2)
             transpose_patches(3)
             add_steps[0](second_chunk)
-            for c in range(N_CHUNKS + 2):
+            for c in range(N_CHUNKS + 1):
                 q = c - 1
                 f = c - 2
                 summing = c < N_CHUNKS
@@ -401,6 +400,7 @@ def tile_qca_operator_deep_pa_t_kernel(tc, x_cat, w1_words, w1_scales, out):
                     quantise(2 * q, 0)
                     multiply(2 * q, 0)
                 if c == 0:
+                    copy_patches(2)
                     add_steps[1](second_chunk)
                 for step, batch in due[0:1]:
                     add_steps[step](batch)
@@ -409,7 +409,7 @@ def tile_qca_operator_deep_pa_t_kernel(tc, x_cat, w1_words, w1_scales, out):
                     quantise(2 * q, 1)
                     multiply(2 * q, 1)
                 for h in range(2):
-                    if ahead and not patches_on_scalar(2 * c + 2 + h):
+                    if ahead and not patches_on_scalar(2 * c + 2 + h) and 2 * c + 2 + h != 2:
                         copy_patches(2 * c + 2 + h)
                     if c == 0:
                         add_steps[2 + h](second_chunk)
@@ -434,8 +434,19 @@ def tile_qca_operator_deep_pa_t_kernel(tc, x_cat, w1_words, w1_scales, out):
                     transpose_patches(2 * c + 5)
                 if ahead:
                     sum_on_tensor_engine(2 * c + 3)
-                if finishing:
-                    for h in range(2):
-                        if f == N_CHUNKS - 1 and not scalar_takes(f):
-                            minus_one(f, h, h + 1)
-                        finish(f, h)
+                if finishing and f < N_CHUNKS - 2:
+                    finish(f, 0)
+                    finish(f, 1)
+            k = N_CHUNKS - 1
+            half = BANK // 2
+            exponential(k, 0)
+            exponential(k, 1, 0, half)
+            exponential(k, 1, half, BANK)
+            finish(k - 1, 0)
+            minus_one(k, 0, BANK)
+            finish(k - 1, 1)
+            finish(k, 0)
+            minus_one(k, BANK, BANK + half)
+            minus_one(k, BANK + half, CHUNK)
+            finish(k, 1, 0, half)
+            finish(k, 1, half, BANK)

@@ -65,6 +65,9 @@ def tile_qca_operator_deep_pa_t_kernel(tc, x_cat, w1_words, w1_scales, out):
         x_pad = keep.tile([P, IMAGES, SIDE, SIDE], BF16, name="x_pad")
         w_codes = keep.tile([P, WORDS, HALVES, 2 * HID], U8, name="w_codes", align_bytes=64)
         w_planes = keep.tile([P, HALVES, HID], U8, name="w_planes", align_bytes=64)
+        warm = keep.tile([P, 1], F32, name="warm")
+        nc.gpsimd.memset(warm[:], 0.0)
+        nc.scalar.activation(out=warm[:], in_=warm[:], func=EXP)
         ident = keep.tile([P, P], BF16, name="ident")
         make_identity(nc, ident[:])
         nc.gpsimd.memset(w_codes[:].rearrange("p h d n -> p (h d n)").bitcast(I32), 0)
@@ -337,12 +340,12 @@ def tile_qca_operator_deep_pa_t_kernel(tc, x_cat, w1_words, w1_scales, out):
             transpose_patches(0)
             transpose_patches(1)
             add_steps[0](first_chunk)
+            add_steps[1](first_chunk)
             copy_patches(0)
             sum_on_tensor_engine(0)
-            add_steps[1](first_chunk)
+            add_steps[2](first_chunk)
             copy_patches(1)
             sum_on_tensor_engine(1)
-            add_steps[2](first_chunk)
             for s in range(STRIPS):
                 copy_strip(0, s, CHUNK_ROWS, SIDE - CHUNK_ROWS, nc.scalar.copy if s < 2 else nc.vector.tensor_copy)
                 if s == 3:
@@ -391,17 +394,20 @@ def tile_qca_operator_deep_pa_t_kernel(tc, x_cat, w1_words, w1_scales, out):
                         repeat_vector_rows(n)
 
                 def strips_due(lo, hi):
-                    if image < IMAGES:
-                        for s in range(STRIPS):
-                            if part == (0 if s < 2 else 1) and lo <= s < hi:
+                    for image in range(1, IMAGES):
+                        for s in range(lo, hi):
+                            start = 0 if image == 1 else CHUNKS_PER_IMAGE * (image - 1) - 2
+                            spread = (0, 0, 1, 1, 1) if image == 1 else (0, 1, 2, 3, 3)
+                            if c == start + spread[s]:
                                 copy_strip(image, s, 0, SIDE)
+
 
                 if quantising:
                     quantise(2 * q, 0)
                     multiply(2 * q, 0)
                 if c == 0:
-                    copy_patches(2)
                     add_steps[1](second_chunk)
+                    copy_patches(2)
                 for step, batch in due[0:1]:
                     add_steps[step](batch)
                 own_rows(0)

from contextlib import ExitStack

import concourse.mybir as mybir
from concourse.masks import make_identity

FLOPS = 2 * 4 * 64 * 64 * 1024 * 128

BF16 = mybir.dt.bfloat16
F32 = mybir.dt.float32
I32 = mybir.dt.int32
U32 = mybir.dt.uint32
U8 = mybir.dt.uint8
FP8X4 = mybir.dt.float8_e4m3fn_x4
FP4X4 = mybir.dt.float4_e2m1fn_x4
ADD = mybir.AluOpType.add
MAX = mybir.AluOpType.max
MIN = mybir.AluOpType.min
MULT = mybir.AluOpType.mult
EXP = mybir.ActivationFunctionType.Exp
RELU = mybir.ActivationFunctionType.Relu

P = 128
PACK = 4
IMAGES = 4
SIDE = 64
WORDS = 2
HALVES = 2
GROUPS = 2
HID = 128

CHUNK_ROWS = 16
CHUNK = CHUNK_ROWS * SIDE
CHUNKS_PER_IMAGE = SIDE // CHUNK_ROWS
N_CHUNKS = IMAGES * CHUNKS_PER_IMAGE
BANK = 512
BANKS_PER_CHUNK = CHUNK // BANK
PITCH = SIDE + 1
BANK_ROWS = BANK // SIDE
PATCH_ROWS = 8
PATCH_COLS = 16
STRIPS = 5
STRIP_STEP = 12
PAIR = 2
BANKS_PER_IMAGE = SIDE // BANK_ROWS
PAIRS = BANKS_PER_IMAGE - 1
PAIR_PIXELS = PAIR * SIDE


def tile_qca_operator_deep_pa_t_kernel(tc, x_cat, w1_words, w1_scales, out):
    nc = tc.nc
    with ExitStack() as stack:
        keep = stack.enter_context(tc.tile_pool(name="keep", bufs=1))
        sums = stack.enter_context(tc.tile_pool(name="sums", bufs=2))
        nbrs = stack.enter_context(tc.tile_pool(name="nbrs", bufs=4))
        strip_pool = stack.enter_context(tc.tile_pool(name="strip_pool", bufs=2))
        patches = stack.enter_context(tc.tile_pool(name="patches", bufs=4))
        moving = stack.enter_context(tc.tile_pool(name="moving", bufs=8))
        packed = stack.enter_context(tc.tile_pool(name="packed", bufs=4))
        tails = stack.enter_context(tc.tile_pool(name="tails", bufs=3))
        results = stack.enter_context(tc.tile_pool(name="results", bufs=8))
        psum_flip = stack.enter_context(tc.psum_pool(name="psum_flip", bufs=2))
        psum_nbr = stack.enter_context(tc.psum_pool(name="psum_nbr", bufs=2))
        psum_acc = stack.enter_context(tc.psum_pool(name="psum_acc", bufs=4))

        x_pad = keep.tile([P, IMAGES, SIDE, SIDE], BF16, name="x_pad")
        w_codes = keep.tile([P, WORDS, HALVES, 2 * HID], U8, name="w_codes", align_bytes=64)
        w_planes = keep.tile([P, HALVES, HID], U8, name="w_planes", align_bytes=64)
        warm = keep.tile([P, 1], F32, name="warm")
        nc.gpsimd.memset(warm[:], 0.0)
        nc.scalar.activation(out=warm[:], in_=warm[:], func=EXP)
        ident = keep.tile([P, P], BF16, name="ident")
        make_identity(nc, ident[:])
        nc.gpsimd.memset(w_codes[:].rearrange("p h d n -> p (h d n)").bitcast(I32), 0)
        nc.gpsimd.memset(w_planes[:].rearrange("p d n -> p (d n)").bitcast(I32), 0)

        def load_rows(b, first, count):
            for g in range(GROUPS):
                nc.sync.dma_start(
                    out=x_pad[64 * g : 64 * (g + 1), b, first : first + count, :].rearrange("c i j -> c (i j)"),
                    in_=x_cat[b, 64 * g : 64 * (g + 1), first : first + count, :].rearrange(
                        "(d m) i j -> m d (i j)", d=HALVES
                    ),
                )

        load_rows(0, 0, CHUNK_ROWS + PAIR)
        load_rows(0, CHUNK_ROWS + PAIR, SIDE // 2 - CHUNK_ROWS)
        load_rows(0, SIDE // 2 + PAIR, SIDE // 2 - PAIR)
        load_rows(1, 0, SIDE)
        for g in range(GROUPS):
            for d in range(HALVES):
                nc.sync.dma_start(
                    out=w_codes[64 * g + d : 64 * (g + 1) : 2, :, d, :].bitcast(I32),
                    in_=w1_words[g, 64 * d : 64 * (d + 1), :].rearrange("(m h) n -> m h n", h=WORDS).bitcast(I32),
                )
        for quadrant in range(4):
            g, f = divmod(quadrant, 2)
            nc.sync.dma_start(
                out=w_planes[32 * quadrant : 32 * quadrant + 4, :, :].bitcast(I32),
                in_=w1_scales[g].rearrange("(d f e) n -> f e d n", d=HALVES, f=2)[f].bitcast(I32),
            )
        for b in range(2, IMAGES):
            load_rows(b, 0, SIDE)

        col_sum = {}
        for banks in (2, 3, 4):
            col_sum[banks] = keep.tile([P, banks * PAIR * PITCH + 2], F32, name="col_sum%d" % banks)
            nc.gpsimd.memset(col_sum[banks][:, 0 : banks * PAIR * PITCH + 1 : PITCH], 0.0)
        ident_pad = keep.tile([P, PATCH_ROWS, PATCH_COLS + 2], BF16, name="ident_pad")
        nc.vector.memset(ident_pad[:], 0.0)
        nc.vector.tensor_copy(
            out=ident_pad[:, :, 1 : PATCH_COLS + 1], in_=ident[:].rearrange("p (i j) -> p i j", j=PATCH_COLS)
        )
        beside = keep.tile([P, PATCH_ROWS, PATCH_COLS], BF16, name="beside")
        nc.vector.tensor_tensor(
            out=beside[:], in0=ident_pad[:, :, 0:PATCH_COLS], in1=ident_pad[:, :, 2 : PATCH_COLS + 2], op=ADD
        )
        around = keep.tile([P, PATCH_ROWS + 2, PATCH_COLS], BF16, name="around")
        nc.vector.memset(around[:], 0.0)
        nc.vector.tensor_tensor(
            out=around[:, 1 : PATCH_ROWS + 1, :], in0=beside[:], in1=ident_pad[:, :, 1 : PATCH_COLS + 1], op=ADD
        )
        outer = keep.tile([P, PATCH_ROWS, PATCH_COLS], BF16, name="outer")
        nc.vector.tensor_tensor(
            out=outer[:], in0=around[:, 0:PATCH_ROWS, :], in1=around[:, 2 : PATCH_ROWS + 2, :], op=ADD
        )
        window = keep.tile([P, PATCH_ROWS, PATCH_COLS], BF16, name="window")
        nc.vector.tensor_tensor(out=window[:], in0=outer[:], in1=beside[:], op=ADD)

        above_below = {}
        left_right = {}
        nbr = {}
        strips = {}
        flipped = {}
        nbr_acc = {}
        xn = {}
        acc = {}
        neg = {}

        def rows_of(flat):
            return flat.rearrange("p (g r j) -> p g r j", r=PAIR, j=SIDE)

        def column_sums(batch, shift):
            banks = batch[2]
            return col_sum[banks][:, shift : shift + banks * PAIR * PITCH].rearrange(
                "p (g r j) -> p g r j", r=PAIR, j=PITCH
            )[:, :, :, 0:SIDE]

        def padded_rows(batch, offset):
            b, first, count = batch
            top = first * BANK_ROWS - 2 + offset
            return x_pad[:, b, top : top + count * BANK_ROWS, :].rearrange("p (g r) j -> p g r j", r=BANK_ROWS)[
                :, :, 0:PAIR, :
            ]

        def add_above_and_below(batch):
            above_below[batch] = sums.tile([P, batch[2] * PAIR_PIXELS], F32, name="above_below")
            nc.vector.tensor_tensor(
                out=rows_of(above_below[batch][:]), in0=padded_rows(batch, 0), in1=padded_rows(batch, 2), op=ADD
            )

        def add_centre(batch):
            nc.vector.tensor_tensor(
                out=column_sums(batch, 1), in0=rows_of(above_below[batch][:]), in1=padded_rows(batch, 1), op=ADD
            )

        def add_left_and_right(batch):
            left_right[batch] = sums.tile([P, batch[2] * PAIR_PIXELS], F32, name="left_right")
            nc.vector.tensor_tensor(
                out=rows_of(left_right[batch][:]), in0=column_sums(batch, 0), in1=column_sums(batch, 2), op=ADD
            )

        def add_up_and_round(batch):
            b, first, count = batch
            if b not in nbr:
                nbr[b] = nbrs.tile([P, PAIRS * PAIR_PIXELS], BF16, name="rounded")
            nc.vector.tensor_tensor(
                out=nbr[b][:, (first - 1) * PAIR_PIXELS : (first - 1 + count) * PAIR_PIXELS],
                in0=left_right[batch][:],
                in1=above_below[batch][:],
                op=ADD,
            )

        add_steps = [add_above_and_below, add_centre, add_left_and_right, add_up_and_round]

        def copy_strip(b, s, first, count, copy=nc.vector.tensor_copy):
            if b not in strips:
                strips[b] = strip_pool.tile([P, STRIPS, SIDE, PATCH_COLS], BF16, name="strips")
            copy(
                out=strips[b][:, s, first : first + count, :],
                in_=x_pad[:, b, first : first + count, s * STRIP_STEP : s * STRIP_STEP + PATCH_COLS],
            )

        def transpose_patches(n):
            b, g = divmod(n, BANKS_PER_IMAGE)
            flipped[n] = psum_flip.tile([P, STRIPS * P], BF16, name="flipped")
            for s in range(STRIPS):
                nc.tensor.transpose(
                    flipped[n][:, s * P : (s + 1) * P],
                    strips[b][:, s, g * BANK_ROWS : g * BANK_ROWS + PATCH_ROWS, :].rearrange("p i j -> p (i j)"),
                    ident[:],
                )

        blocks_of = {}

        def tensor_rows(n):
            g = n % BANKS_PER_IMAGE
            return (0 if g == 0 else 1, BANK_ROWS if g == BANKS_PER_IMAGE - 1 else BANK_ROWS - 1)

        def patches_on_scalar(n):
            return n > 3

        def tensor_rows_on_vector(n):
            return False

        def repeats_on_vector(n):
            return n % 2 == 1 or n >= 28

        def copy_patches(n):
            blocks_of[n] = patches.tile([P, STRIPS * P], BF16, name="blocks")
            copy = nc.scalar.copy if patches_on_scalar(n) else nc.vector.tensor_copy
            copy(out=blocks_of[n][:], in_=flipped[n][:])

        def sum_on_tensor_engine(n):
            blocks = blocks_of[n]
            nbr_acc[n] = psum_nbr.tile([P, BANK_ROWS, SIDE], F32, name="nbr_acc")
            top, end = tensor_rows(n)
            for s in range(STRIPS):
                lo = 0 if s == 0 else 1
                hi = PATCH_COLS if s == STRIPS - 1 else STRIP_STEP + 1
                nc.tensor.matmul(
                    out=nbr_acc[n][:, top:end, s * STRIP_STEP + lo : s * STRIP_STEP + hi],
                    lhsT=blocks[:, s * P : (s + 1) * P],
                    rhs=window[:, top:end, lo:hi],
                    start=True,
                    stop=True,
                )


        def xn_tiles(n):
            xn[n] = moving.tile([P, BANK * PACK], BF16, name="xn", align_bytes=64)

        def words_of_rows(n):
            return xn[n][:].rearrange("p (i j t) -> p i j t", j=SIDE, t=PACK)

        def repeat_tensor_rows(n):
            top, end = tensor_rows(n)
            copy = nc.vector.tensor_copy if tensor_rows_on_vector(n) else nc.scalar.copy
            copy(
                out=words_of_rows(n)[:, top:end],
                in_=nbr_acc[n][:, top:end, :].unsqueeze(3).to_broadcast([P, end - top, SIDE, PACK]),
            )

        def repeat_vector_rows(n):
            copy = nc.vector.tensor_copy if repeats_on_vector(n) else nc.scalar.copy
            b, g = divmod(n, BANKS_PER_IMAGE)
            if g == 0:
                rows, first, count = slice(BANK_ROWS - 1, BANK_ROWS), 0, 1
            elif g == BANKS_PER_IMAGE - 1:
                rows, first, count = slice(0, 1), 2 * PAIRS - 1, 1
            else:
                rows, first, count = slice(0, BANK_ROWS, BANK_ROWS - 1), 2 * g - 1, 2
            copy(
                out=words_of_rows(n)[:, rows],
                in_=nbr[b][:, first * SIDE : (first + count) * SIDE]
                .rearrange("p (i j) -> p i j", j=SIDE)
                .unsqueeze(3)
                .to_broadcast([P, count, SIDE, PACK]),
            )

        codes = {}
        planes = {}

        def quantise(n, w):
            if w == 0:
                codes[n] = packed.tile([P, WORDS * BANK], U32, name="codes", align_bytes=64)
                planes[n] = packed.tile([P, WORDS * BANK], U8, name="planes", align_bytes=64)
            part = slice(w * BANK, (w + 1) * BANK)
            nc.vector.quantize_mx(out=codes[n][:, part].bitcast(FP8X4), scales=planes[n][:, part], in_=xn[n][:])

        def multiply(n, w):
            if w == 0:
                acc[n] = psum_acc.tile([HID, BANK], F32, name="acc")
            part = slice(w * BANK, (w + 1) * BANK)
            for d in range(HALVES):
                nc.tensor.matmul_mx(
                    out=acc[n][:],
                    lhsT=w_codes[:, w, d, :].bitcast(FP4X4),
                    lhsT_scale=w_planes[:, d, :],
                    rhs=codes[n][:, part].bitcast(FP8X4),
                    rhs_scale=planes[n][:, part],
                    start=(w == 0 and d == 0),
                    stop=(w == WORDS - 1 and d == HALVES - 1),
                )


        def exponential(k, h, lo=0, hi=BANK):
            if h == 0:
                neg[k] = tails.tile([HID, CHUNK], F32, name="neg")
            nc.scalar.activation(
                out=neg[k][:, h * BANK + lo : h * BANK + hi], in_=acc[2 * k + h][:, lo:hi], func=EXP
            )

        def minus_one(k, lo=0, hi=CHUNK):
            part = neg[k][:, lo:hi]
            nc.vector.tensor_scalar(out=part, in0=part, scalar1=1.0, scalar2=-1.0, op0=MIN, op1=ADD)

        def scalar_takes(k):
            return k == N_CHUNKS - 2

        def one_minus(k, h):
            part = neg[k][:, h * BANK : (h + 1) * BANK]
            nc.scalar.activation(out=part, in_=part, func=RELU, bias=1.0, scale=-1.0)

        def finish(k, h, lo=0, hi=BANK):
            n = 2 * k + h
            res = results.tile([HID, hi - lo], F32, name="res")
            nc.vector.scalar_tensor_tensor(
                out=res[:],
                in0=neg[k][:, h * BANK + lo : h * BANK + hi],
                scalar=-1.0 if scalar_takes(k) else 1.0,
                in1=acc[n][:, lo:hi],
                op0=MULT,
                op1=MAX,
            )
            b, g = divmod(n, BANKS_PER_IMAGE)
            nc.sync.dma_start(
                out=out[b, :, g * BANK_ROWS : (g + 1) * BANK_ROWS, :].rearrange("o i j -> o (i j)")[:, lo:hi], in_=res[:]
            )

        def xn_tile(n):
            if n not in xn:
                xn[n] = moving.tile([P, BANK * PACK], BF16, name="xn", align_bytes=64)

        with tc.manual_schedule():
            first_chunk = (0, 1, 2)
            second_chunk = (0, 3, 2)
            halves = [(1, 4), (5, 3)]
            for s in range(STRIPS):
                copy_strip(0, s, 0, CHUNK_ROWS)
            transpose_patches(0)
            transpose_patches(1)
            add_steps[0](first_chunk)
            add_steps[1](first_chunk)
            copy_patches(0)
            sum_on_tensor_engine(0)
            add_steps[2](first_chunk)
            copy_patches(1)
            sum_on_tensor_engine(1)
            for s in range(STRIPS):
                copy_strip(0, s, CHUNK_ROWS, SIDE - CHUNK_ROWS, nc.scalar.copy if s < 2 else nc.vector.tensor_copy)
                if s == 3:
                    add_steps[3](first_chunk)
            transpose_patches(2)
            transpose_patches(3)
            add_steps[0](second_chunk)
            for c in range(N_CHUNKS + 1):
                q = c - 1
                f = c - 2
                summing = c < N_CHUNKS
                ahead = c + 1 < N_CHUNKS
                quantising = 0 <= q < N_CHUNKS
                finishing = 0 <= f
                half, stage = divmod(c + 2, 2)
                b, second = divmod(half, 2)
                due = []
                if b < IMAGES:
                    due = [(2 * stage + i, (b,) + halves[second]) for i in range(2)]
                for h in range(2):
                    n = 2 * c + h
                    if finishing:
                        exponential(f, h)
                        if scalar_takes(f):
                            one_minus(f, h)
                    if ahead and patches_on_scalar(n + 2):
                        copy_patches(n + 2)
                    if summing:
                        xn_tile(n)
                        if not tensor_rows_on_vector(n):
                            repeat_tensor_rows(n)
                        if c > 0 and not repeats_on_vector(n):
                            repeat_vector_rows(n)
                if c == 0:
                    repeat_vector_rows(0)
                    repeat_vector_rows(1)

                part = c % CHUNKS_PER_IMAGE
                image = c // CHUNKS_PER_IMAGE + 1

                def own_rows(h):
                    n = 2 * c + h
                    if summing and tensor_rows_on_vector(n):
                        repeat_tensor_rows(n)
                    if summing and c > 0 and repeats_on_vector(n):
                        repeat_vector_rows(n)

                def strips_due(lo, hi):
                    for image in range(1, IMAGES):
                        for s in range(lo, hi):
                            start = 0 if image == 1 else CHUNKS_PER_IMAGE * (image - 1) - 2
                            spread = (0, 0, 1, 1, 1) if image == 1 else (0, 1, 2, 3, 3)
                            if c == start + spread[s]:
                                copy_strip(image, s, 0, SIDE)


                if quantising:
                    quantise(2 * q, 0)
                    multiply(2 * q, 0)
                if c == 0:
                    add_steps[1](second_chunk)
                    copy_patches(2)
                for step, batch in due[0:1]:
                    add_steps[step](batch)
                own_rows(0)
                if quantising:
                    quantise(2 * q, 1)
                    multiply(2 * q, 1)
                for h in range(2):
                    if ahead and not patches_on_scalar(2 * c + 2 + h) and 2 * c + 2 + h != 2:
                        copy_patches(2 * c + 2 + h)
                    if c == 0:
                        add_steps[2 + h](second_chunk)
                if ahead:
                    sum_on_tensor_engine(2 * c + 2)
                if c + 2 < N_CHUNKS:
                    transpose_patches(2 * c + 4)
                strips_due(0, 3)
                for step, batch in due[1:2]:
                    add_steps[step](batch)
                if quantising:
                    quantise(2 * q + 1, 0)
                    multiply(2 * q + 1, 0)
                if finishing and f < N_CHUNKS - 1 and not scalar_takes(f):
                    minus_one(f)
                own_rows(1)
                if quantising:
                    quantise(2 * q + 1, 1)
                    multiply(2 * q + 1, 1)
                strips_due(3, STRIPS)
                if c + 2 < N_CHUNKS:
                    transpose_patches(2 * c + 5)
                if ahead:
                    sum_on_tensor_engine(2 * c + 3)
                if finishing and f < N_CHUNKS - 2:
                    finish(f, 0)
                    finish(f, 1)
            k = N_CHUNKS - 1
            half = BANK // 2
            exponential(k, 0)
            exponential(k, 1, 0, half)
            exponential(k, 1, half, BANK)
            finish(k - 1, 0)
            minus_one(k, 0, BANK)
            finish(k - 1, 1)
            finish(k, 0)
            minus_one(k, BANK, BANK + half)
            minus_one(k, BANK + half, CHUNK)
            finish(k, 1, 0, half)
            finish(k, 1, half, BANK)
